import numpy as np
import ml_dtypes


def mxq(x, axis, fmt="e4m3"):
    dtype, down = {"e4m3": (ml_dtypes.float8_e4m3fn, 7), "e5m2": (ml_dtypes.float8_e5m2, 14)}[fmt]
    v = np.moveaxis(np.asarray(x, np.float32).astype(ml_dtypes.bfloat16).astype(np.float64), axis, -1)
    blocks = v.reshape(v.shape[:-1] + (-1, 32))
    amax = np.abs(blocks).max(-1, keepdims=True)
    byte = np.maximum(np.where(amax > 0, np.frexp(amax)[1] - 1 + 127, 0) - down, 1)
    scale = np.exp2(byte - 127.0)
    codes = (blocks / scale).astype(np.float32).astype(dtype).astype(np.float64)
    return np.moveaxis((codes * scale).reshape(v.shape), -1, axis)


WIDE = False


def mx_kscale(k):
    if not WIDE:
        return np.ones(k)
    levels = np.array([10, -10, 5, -5, 0])
    a = np.random.permutation(np.resize(levels, k // 512 * 4)).reshape(k // 512, 4)
    idx = np.arange(k)
    return np.exp2(a[idx // 512, idx % 128 // 32])


BF16 = ml_dtypes.bfloat16


def bf(x):
    return np.asarray(x, np.float32).astype(BF16)


def f64(x):
    return np.asarray(x).astype(np.float64)


E2M1 = np.array([0.0, 0.5, 1.0, 1.5, 2.0, 3.0, 4.0, 6.0, -0.0, -0.5, -1.0, -1.5, -2.0, -3.0, -4.0, -6.0])


def pack_weight(w, fmt):
    k, n = w.shape
    w = f64(bf(w)).reshape(k // 32, 32, n)
    amax = np.abs(w).max(1)
    if fmt == "e4m3":
        byte = np.frexp(amax)[1] - 1 + 127 - 7
    else:
        mant, ex = np.frexp(amax / 6.0)
        byte = np.where(mant > 0.5, ex, ex - 1) + 127
    byte = np.clip(np.where(amax > 0, byte, 1), 1, 254)
    scaled = (w * np.exp2(127.0 - byte)[:, None, :]).reshape(k, n).astype(np.float32)
    by_word = np.ascontiguousarray(scaled.reshape(k // 512, 128, 4, n).transpose(0, 1, 3, 2))
    if fmt == "e4m3":
        words = by_word.astype(ml_dtypes.float8_e4m3fn).view(np.uint8)
    else:
        c = by_word.astype(ml_dtypes.float4_e2m1fn).view(np.uint8) & 0xF
        words = c[..., 0::2] | (c[..., 1::2] << 4)
    return np.ascontiguousarray(words), np.ascontiguousarray(byte.astype(np.uint8).reshape(k // 512, 16, n))


def unpack_weight(words, scales, fmt):
    g, p, n, _ = words.shape
    if fmt == "e4m3":
        vals = np.ascontiguousarray(words).view(ml_dtypes.float8_e4m3fn).astype(np.float64)
    else:
        nib = np.empty((g, p, n, 4), np.uint8)
        nib[..., 0::2] = words & 0xF
        nib[..., 1::2] = words >> 4
        vals = E2M1[nib]
    vals = vals * np.repeat(np.exp2(scales.astype(np.float64) - 127.0), 8, axis=1)[..., None]
    return vals.transpose(0, 1, 3, 2).reshape(g * 512, n)

def pack4(w):
    words, scales = pack_weight(w, "e2m1")
    return words.reshape(words.shape[0], 128, -1), scales


def unpack4(words, scales):
    return unpack_weight(words.reshape(words.shape[0], 128, -1, 2), scales, "e2m1")


B, N, D, H = 64, 16, 128, 1024


def setup_inputs():
    t = mx_kscale(H)
    xi_p = bf(np.random.standard_normal((B, N, H)) * 0.7 * t)
    xj_p = bf(np.random.standard_normal((B, N, H)) * 0.7 * t)
    node_mask = bf(np.random.uniform(size=(B, N)) < 0.9)
    mb1 = bf(np.random.standard_normal(H) * 0.2 * t)
    mw2_words, mw2_scales = pack4(np.random.standard_normal((H, D)) * 0.5 / np.sqrt(H) / t[:, None])
    mb2 = bf(np.random.standard_normal(D) * 0.1)
    return {
        "xi_p": xi_p,
        "xj_p": xj_p,
        "node_mask": node_mask,
        "mb1": mb1,
        "mw2_words": mw2_words,
        "mw2_scales": mw2_scales,
        "mb2": mb2,
    }


def reference(xi_p, xj_p, node_mask, mb1, mw2_words, mw2_scales, mb2):
    mask = f64(node_mask)[..., None]
    h = np.maximum(f64(xi_p)[:, :, None, :] + f64(xj_p)[:, None, :, :] + f64(mb1), 0.0)
    msgs = np.maximum((mxq(h, 3, "e4m3") @ unpack4(mw2_words, mw2_scales)) + f64(mb2), 0.0)
    msgs = msgs * mask[:, None]
    return msgs.sum(axis=2)

@@ -1,0 +1,322 @@
+from contextlib import ExitStack
+
+import concourse.mybir as mybir
+from concourse.masks import make_identity
+
+F32 = mybir.dt.float32
+BF16 = mybir.dt.bfloat16
+I32 = mybir.dt.int32
+U32 = mybir.dt.uint32
+U8 = mybir.dt.uint8
+FP8X4 = mybir.dt.float8_e4m3fn_x4
+FP4X4 = mybir.dt.float4_e2m1fn_x4
+ALU = mybir.AluOpType
+ACT = mybir.ActivationFunctionType
+AXIS = mybir.AxisListType
+
+GRAPHS = 64
+NODES = 16
+HIDDEN = 1024
+OUT_DIM = 128
+
+P = 128
+PACK = 4
+K_PASS = P * PACK
+PASSES = HIDDEN // K_PASS
+PLANES = PASSES * PACK
+
+GROUP = 4
+GROUP_NODES = GROUP * NODES
+GROUP_PAIRS = GROUP * NODES * NODES
+N_GROUPS = GRAPHS // GROUP
+PAIR_TILE = P
+TILE_RECEIVERS = PAIR_TILE // NODES
+PAIR_TILES = GROUP_PAIRS // PAIR_TILE
+BANK_TILES = 4
+NODE_TILE = P
+TILE_GRAPHS = NODE_TILE // NODES
+N_NODE_TILES = GRAPHS * NODES // NODE_TILE
+XI_SLOTS = 4
+
+FLOPS = 2 * GRAPHS * NODES * NODES * HIDDEN * OUT_DIM
+
+
+def tile_graphdynamics_pa_t_kernel(
+    tc, xi_p, xj_p, node_mask, mb1, mw2_words, mw2_scales, mb2, out
+):
+    nc = tc.nc
+    xi_rows = xi_p.rearrange("b n h -> (b n) h")
+    xj_rows = xj_p.rearrange("b n h -> (b n) h")
+    out_rows = out.rearrange("b n d -> (b n) d")
+
+    with ExitStack() as stack:
+        keep = stack.enter_context(tc.tile_pool(name="keep", bufs=1))
+        work = stack.enter_context(tc.tile_pool(name="work", bufs=2))
+        deep = stack.enter_context(tc.tile_pool(name="deep", bufs=4))
+        ps_recv = stack.enter_context(tc.psum_pool(name="ps_recv", bufs=2))
+        ps_send = stack.enter_context(tc.psum_pool(name="ps_send", bufs=1))
+        ps_acc = stack.enter_context(tc.psum_pool(name="ps_acc", bufs=2))
+        ps_sum = stack.enter_context(tc.psum_pool(name="ps_sum", bufs=2))
+        ps_misc = stack.enter_context(tc.psum_pool(name="ps_misc", bufs=1))
+        stack.enter_context(tc.manual_schedule())
+
+        ident_bf = keep.tile([P, P], BF16, name="ident_bf")
+        ident_f32 = keep.tile([P, P], F32, name="ident_f32")
+        pick = keep.tile([P, GROUP_NODES], BF16, name="pick")
+        xi_aug = keep.tile([P, XI_SLOTS, HIDDEN], BF16, name="xi_aug")
+        xj_sb = keep.tile([P, N_NODE_TILES, HIDDEN], BF16, name="xj_sb")
+        w_words = keep.tile([P, PASSES, 2 * OUT_DIM], U8, name="w_words", align_bytes=64)
+        w_scales = keep.tile([P, PASSES, OUT_DIM], U8, name="w_scales", align_bytes=64)
+        mask_rows = keep.tile([P, NODES], BF16, name="mask_rows")
+        mask_wide = keep.tile([P, TILE_RECEIVERS, NODES], BF16, name="mask_wide")
+        bias_bf = keep.tile([P, OUT_DIM], BF16, name="bias_bf")
+        bias_rows = keep.tile([P, OUT_DIM], F32, name="bias_rows")
+        neg_bias = keep.tile([P, OUT_DIM], F32, name="neg_bias")
+        same_receiver = keep.tile([P, TILE_RECEIVERS], F32, name="same_receiver")
+        sel = keep.tile([P, GRAPHS, TILE_RECEIVERS], F32, name="sel")
+        bias_share = keep.tile([P, GRAPHS, TILE_RECEIVERS], F32, name="bias_share")
+
+        recv_of = {}
+        send_of = {}
+        pre_of = {}
+        h_of = {}
+        codes_of = {}
+        scales_of = {}
+        acc_of = {}
+        floor_of = {}
+        sums_of = {}
+
+        def load_receivers(grp):
+            nc.sync.dma_start(
+                out=xi_aug[0:GROUP_NODES, grp % XI_SLOTS, :],
+                in_=xi_rows[grp * GROUP_NODES : (grp + 1) * GROUP_NODES, :],
+            )
+
+        def load_senders(nt):
+            nc.sync.dma_start(
+                out=xj_sb[:, nt, :], in_=xj_rows[nt * NODE_TILE : (nt + 1) * NODE_TILE, :]
+            )
+
+        nc.vector.memset(xi_aug[GROUP_NODES:P, :, :].bitcast(I32), 0)
+        nc.vector.memset(w_scales[:].bitcast(I32), 0)
+        nc.vector.memset(mask_rows[:], 0.0)
+
+        nc.scalar.dma_start(
+            out=xi_aug[GROUP_NODES : GROUP_NODES + 1, :, :],
+            in_=mb1.unsqueeze(0).unsqueeze(0).broadcast_to([1, XI_SLOTS, HIDDEN]),
+        )
+        nc.scalar.dma_start(out=bias_bf[:], in_=mb2.partition_broadcast(P))
+        nc.scalar.dma_start(out=mask_rows[0:GRAPHS, :], in_=node_mask)
+
+        load_receivers(0)
+        load_senders(0)
+        load_receivers(1)
+        for g in range(PASSES):
+            nc.sync.dma_start(out=w_words[:, g, :].bitcast(I32), in_=mw2_words[g].bitcast(I32))
+        for quad in range(4):
+            nc.sync.dma_start(
+                out=w_scales[32 * quad : 32 * quad + 4, :, :].bitcast(I32),
+                in_=mw2_scales[:, 4 * quad : 4 * quad + 4, :]
+                .rearrange("g q n -> q g n")
+                .bitcast(I32),
+            )
+        load_receivers(2)
+        load_receivers(3)
+        for nt in range(1, N_NODE_TILES):
+            load_senders(nt)
+
+        make_identity(nc, ident_bf[:])
+        make_identity(nc, ident_f32[:])
+        nc.vector.tensor_copy(out=pick[:], in_=ident_bf[:, 0:GROUP_NODES])
+        nc.vector.memset(pick[GROUP_NODES : GROUP_NODES + 1, :], 1.0)
+
+        def prepare_receivers(grp):
+            recv = ps_recv.tile([P, PLANES, GROUP_NODES], F32, name="recv")
+            recv_of[grp] = recv
+            for plane in range(PLANES):
+                g, t = divmod(plane, PACK)
+                nc.tensor.matmul(
+                    out=recv[:, plane, :],
+                    lhsT=xi_aug[:, grp % XI_SLOTS, K_PASS * g + t : K_PASS * (g + 1) : PACK],
+                    rhs=pick[:],
+                    start=True,
+                    stop=True,
+                )
+            if grp + XI_SLOTS < N_GROUPS:
+                load_receivers(grp + XI_SLOTS)
+
+        def prepare_senders(nt):
+            words = xj_sb[:, nt, :].bitcast(F32)
+            turned = ps_send.tile([P, PASSES * 2, NODE_TILE], F32, name="turned")
+            for half_plane in range(PASSES * 2):
+                g, u = divmod(half_plane, 2)
+                nc.tensor.transpose(
+                    out=turned[:, half_plane, :],
+                    in_=words[:, (K_PASS // 2) * g + u : (K_PASS // 2) * (g + 1) : 2],
+                    identity=ident_f32[:],
+                )
+            send = work.tile([P, PASSES, NODE_TILE, PACK], BF16, name="send")
+            send_of[nt] = send
+            nc.scalar.copy(
+                out=send[:]
+                .rearrange("p g n t -> p (g n t)")
+                .bitcast(F32)
+                .rearrange("p (g n u) -> p g n u", g=PASSES, u=2),
+                in_=turned[:].rearrange("p (g u) n -> p g n u", u=2),
+            )
+
+        def add(grp, g):
+            shape = [P, GROUP, NODES, NODES, PACK]
+            first = (grp % 2) * GROUP_NODES
+            receivers = (
+                recv_of[grp][:, PACK * g : PACK * (g + 1), :]
+                .rearrange("p t (b i) -> p b i t", b=GROUP)
+                .unsqueeze(3)
+                .broadcast_to(shape)
+            )
+            senders = (
+                send_of[grp // 2][:, g, first : first + GROUP_NODES, :]
+                .rearrange("p (b j) t -> p b j t", b=GROUP)
+                .unsqueeze(2)
+                .broadcast_to(shape)
+            )
+            pre = work.tile([P, GROUP_PAIRS * PACK], BF16, name="pre")
+            pre_of[(grp, g)] = pre
+            nc.vector.tensor_tensor(
+                out=pre[:].rearrange("p (b i j t) -> p b i j t", b=GROUP, i=NODES, j=NODES),
+                in0=receivers,
+                in1=senders,
+                op=ALU.add,
+            )
+
+        def relu(grp, g):
+            h = work.tile([P, GROUP_PAIRS * PACK], BF16, name="h", align_bytes=64)
+            h_of[(grp, g)] = h
+            nc.scalar.activation(out=h[:], in_=pre_of[(grp, g)][:], func=ACT.Relu)
+
+        def quantise(grp, g):
+            codes = deep.tile([P, GROUP_PAIRS], U32, name="codes", align_bytes=64)
+            scales = deep.tile([P, GROUP_PAIRS], U8, name="scales", align_bytes=64)
+            codes_of[(grp, g)] = codes
+            scales_of[(grp, g)] = scales
+            nc.vector.quantize_mx(out=codes[:].bitcast(FP8X4), scales=scales[:], in_=h_of[(grp, g)][:])
+
+        def multiply(grp):
+            for bank in range(PAIR_TILES // BANK_TILES):
+                acc = ps_acc.tile([P, BANK_TILES, OUT_DIM], F32, name="acc")
+                acc_of[(grp, bank)] = acc
+                for c in range(BANK_TILES):
+                    first = (bank * BANK_TILES + c) * PAIR_TILE
+                    for g in range(PASSES):
+                        nc.tensor.matmul_mx(
+                            out=acc[:, c, :],
+                            lhsT=codes_of[(grp, g)][:, first : first + PAIR_TILE].bitcast(FP8X4),
+                            lhsT_scale=scales_of[(grp, g)][:, first : first + PAIR_TILE],
+                            rhs=w_words[:, g, :].bitcast(FP4X4),
+                            rhs_scale=w_scales[:, g, :],
+                            start=(g == 0),
+                            stop=(g == PASSES - 1),
+                        )
+
+        def leave_psum(grp):
+            for bank in range(PAIR_TILES // BANK_TILES):
+                floored = deep.tile([P, BANK_TILES, OUT_DIM], F32, name="floored")
+                floor_of[(grp, bank)] = floored
+                nc.vector.tensor_tensor(
+                    out=floored[:],
+                    in0=acc_of[(grp, bank)][:],
+                    in1=neg_bias[:].unsqueeze(1).broadcast_to([P, BANK_TILES, OUT_DIM]),
+                    op=ALU.max,
+                )
+
+        def sum_senders(grp):
+            nt = grp // 2
+            if grp % 2 == 0:
+                sums_of[nt] = ps_sum.tile([P, NODE_TILE], F32, name="sums")
+            for tile in range(PAIR_TILES):
+                bank, c = divmod(tile, BANK_TILES)
+                first = ((grp % 2) * PAIR_TILES + tile) * TILE_RECEIVERS
+                nc.tensor.matmul(
+                    out=sums_of[nt][:, first : first + TILE_RECEIVERS],
+                    lhsT=floor_of[(grp, bank)][:, c, :],
+                    rhs=sel[:, grp * GROUP + tile // 2, :],
+                    start=True,
+                    stop=True,
+                )
+
+        def build_selection():
+            nc.vector.tensor_copy(out=bias_rows[:], in_=bias_bf[:])
+            nc.vector.tensor_scalar_mul(out=neg_bias[:], in0=bias_bf[:], scalar1=-1.0)
+            nc.vector.tensor_copy(
+                out=mask_wide[:],
+                in_=mask_rows[:].unsqueeze(1).broadcast_to([P, TILE_RECEIVERS, NODES]),
+            )
+            mask_turned = ps_misc.tile([P, P], BF16, name="mask_turned", tag="misc")
+            nc.tensor.transpose(
+                out=mask_turned[:], in_=mask_wide[:].rearrange("p r j -> p (r j)"), identity=ident_bf[:]
+            )
+            nc.vector.tensor_reduce(
+                out=same_receiver[:],
+                in_=ident_f32[:].rearrange("p (i j) -> p i j", j=NODES),
+                axis=AXIS.X,
+                op=ALU.add,
+            )
+            nc.vector.tensor_tensor(
+                out=sel[:],
+                in0=mask_turned[:, 0:GRAPHS].unsqueeze(2).broadcast_to([P, GRAPHS, TILE_RECEIVERS]),
+                in1=same_receiver[:].unsqueeze(1).broadcast_to([P, GRAPHS, TILE_RECEIVERS]),
+                op=ALU.mult,
+            )
+            share = ps_misc.tile([P, GRAPHS * TILE_RECEIVERS], F32, name="share", tag="misc")
+            nc.tensor.matmul(
+                out=share[:],
+                lhsT=bias_rows[:],
+                rhs=sel[:].rearrange("p b i -> p (b i)"),
+                start=True,
+                stop=True,
+            )
+            nc.scalar.copy(out=bias_share[:].rearrange("p b i -> p (b i)"), in_=share[:])
+
+        def finish(nt):
+            halves = NODES // TILE_RECEIVERS
+            shape = [P, TILE_GRAPHS, halves, TILE_RECEIVERS]
+            total = work.tile([P, NODE_TILE], F32, name="total")
+            nc.vector.tensor_tensor(
+                out=total[:].rearrange("p (b s i) -> p b s i", b=TILE_GRAPHS, s=halves),
+                in0=sums_of[nt][:].rearrange("p (b s i) -> p b s i", b=TILE_GRAPHS, s=halves),
+                in1=bias_share[:, nt * TILE_GRAPHS : (nt + 1) * TILE_GRAPHS, :]
+                .unsqueeze(2)
+                .broadcast_to(shape),
+                op=ALU.add,
+            )
+            turned_out = ps_misc.tile([P, OUT_DIM], F32, name="turned_out", tag="misc")
+            nc.tensor.transpose(out=turned_out[:], in_=total[:], identity=ident_f32[:])
+            result = work.tile([P, OUT_DIM], F32, name="result")
+            nc.scalar.copy(out=result[:], in_=turned_out[:])
+            nc.sync.dma_start(out=out_rows[nt * NODE_TILE : (nt + 1) * NODE_TILE, :], in_=result[:])
+
+        prepare_receivers(0)
+        prepare_senders(0)
+        for step in range(N_GROUPS + 1):
+            if step + 1 < N_GROUPS:
+                prepare_receivers(step + 1)
+                if (step + 1) % 2 == 0:
+                    prepare_senders((step + 1) // 2)
+            if step < N_GROUPS:
+                add(step, 0)
+                relu(step, 0)
+            if step >= 3 and step % 2 == 1:
+                finish((step - 3) // 2)
+            if step >= 1:
+                quantise(step - 1, 1)
+                multiply(step - 1)
+            if step < N_GROUPS:
+                add(step, 1)
+                relu(step, 1)
+                quantise(step, 0)
+            if step == 0:
+                build_selection()
+            if step >= 1:
+                leave_psum(step - 1)
+                sum_senders(step - 1)
+        finish(N_NODE_TILES - 1)

@@ -37,6 +37,10 @@ NODE_TILE = P
 TILE_GRAPHS = NODE_TILE // NODES
 N_NODE_TILES = GRAPHS * NODES // NODE_TILE
 XI_SLOTS = 4
+POOL_GRAPHS = 1
+POOL_NODES = POOL_GRAPHS * NODES
+VECTOR_GRAPHS = GROUP - POOL_GRAPHS
+VECTOR_NODES = VECTOR_GRAPHS * NODES
 
 FLOPS = 2 * GRAPHS * NODES * NODES * HIDDEN * OUT_DIM
 
@@ -77,6 +81,7 @@ def tile_graphdynamics_pa_t_kernel(
         bias_share = keep.tile([P, GRAPHS, TILE_RECEIVERS], F32, name="bias_share")
 
         recv_of = {}
+        recv_copy_of = {}
         send_of = {}
         pre_of = {}
         h_of = {}
@@ -142,6 +147,12 @@ def tile_graphdynamics_pa_t_kernel(
                     start=True,
                     stop=True,
                 )
+            recv_copy = work.tile([P, PASSES, POOL_NODES, PACK], F32, name="recv_copy")
+            recv_copy_of[grp] = recv_copy
+            nc.scalar.copy(
+                out=recv_copy[:],
+                in_=recv[:, :, VECTOR_NODES:GROUP_NODES].rearrange("p (g t) n -> p g n t", t=PACK),
+            )
             if grp + XI_SLOTS < N_GROUPS:
                 load_receivers(grp + XI_SLOTS)
 
@@ -166,26 +177,31 @@ def tile_graphdynamics_pa_t_kernel(
             )
 
         def add(grp, g):
-            shape = [P, GROUP, NODES, NODES, PACK]
             first = (grp % 2) * GROUP_NODES
-            receivers = (
-                recv_of[grp][:, PACK * g : PACK * (g + 1), :]
-                .rearrange("p t (b i) -> p b i t", b=GROUP)
-                .unsqueeze(3)
-                .broadcast_to(shape)
+            senders = send_of[grp // 2][:, g, first : first + GROUP_NODES, :].rearrange(
+                "p (b j) t -> p b j t", b=GROUP
             )
-            senders = (
-                send_of[grp // 2][:, g, first : first + GROUP_NODES, :]
-                .rearrange("p (b j) t -> p b j t", b=GROUP)
-                .unsqueeze(2)
-                .broadcast_to(shape)
-            )
-            pre = work.tile([P, GROUP_PAIRS * PACK], BF16, name="pre")
+            pre = deep.tile([P, GROUP_PAIRS * PACK], BF16, name="pre")
             pre_of[(grp, g)] = pre
+            pairs = pre[:].rearrange("p (b i j t) -> p b i j t", b=GROUP, i=NODES, j=NODES)
+            shape = [P, POOL_GRAPHS, NODES, NODES, PACK]
+            nc.gpsimd.tensor_tensor(
+                out=pairs[:, VECTOR_GRAPHS:GROUP],
+                in0=recv_copy_of[grp][:, g, :, :]
+                .rearrange("p (b i) t -> p b i t", b=POOL_GRAPHS)
+                .unsqueeze(3)
+                .broadcast_to(shape),
+                in1=senders[:, VECTOR_GRAPHS:GROUP].unsqueeze(2).broadcast_to(shape),
+                op=ALU.add,
+            )
+            shape = [P, VECTOR_GRAPHS, NODES, NODES, PACK]
             nc.vector.tensor_tensor(
-                out=pre[:].rearrange("p (b i j t) -> p b i j t", b=GROUP, i=NODES, j=NODES),
-                in0=receivers,
-                in1=senders,
+                out=pairs[:, 0:VECTOR_GRAPHS],
+                in0=recv_of[grp][:, PACK * g : PACK * (g + 1), 0:VECTOR_NODES]
+                .rearrange("p t (b i) -> p b i t", b=VECTOR_GRAPHS)
+                .unsqueeze(3)
+                .broadcast_to(shape),
+                in1=senders[:, 0:VECTOR_GRAPHS].unsqueeze(2).broadcast_to(shape),
                 op=ALU.add,
             )
 

@@ -82,6 +82,7 @@ def tile_graphdynamics_pa_t_kernel(
 
         recv_of = {}
         recv_copy_of = {}
+        turned_of = {}
         send_of = {}
         pre_of = {}
         h_of = {}
@@ -147,18 +148,23 @@ def tile_graphdynamics_pa_t_kernel(
                     start=True,
                     stop=True,
                 )
+            if grp + XI_SLOTS < N_GROUPS:
+                load_receivers(grp + XI_SLOTS)
+
+        def copy_receivers(grp):
             recv_copy = work.tile([P, PASSES, POOL_NODES, PACK], F32, name="recv_copy")
             recv_copy_of[grp] = recv_copy
             nc.scalar.copy(
                 out=recv_copy[:],
-                in_=recv[:, :, VECTOR_NODES:GROUP_NODES].rearrange("p (g t) n -> p g n t", t=PACK),
+                in_=recv_of[grp][:, :, VECTOR_NODES:GROUP_NODES].rearrange(
+                    "p (g t) n -> p g n t", t=PACK
+                ),
             )
-            if grp + XI_SLOTS < N_GROUPS:
-                load_receivers(grp + XI_SLOTS)
 
-        def prepare_senders(nt):
+        def turn_senders(nt):
             words = xj_sb[:, nt, :].bitcast(F32)
             turned = ps_send.tile([P, PASSES * 2, NODE_TILE], F32, name="turned")
+            turned_of[nt] = turned
             for half_plane in range(PASSES * 2):
                 g, u = divmod(half_plane, 2)
                 nc.tensor.transpose(
@@ -166,6 +172,8 @@ def tile_graphdynamics_pa_t_kernel(
                     in_=words[:, (K_PASS // 2) * g + u : (K_PASS // 2) * (g + 1) : 2],
                     identity=ident_f32[:],
                 )
+
+        def copy_senders(nt):
             send = work.tile([P, PASSES, NODE_TILE, PACK], BF16, name="send")
             send_of[nt] = send
             nc.scalar.copy(
@@ -173,35 +181,42 @@ def tile_graphdynamics_pa_t_kernel(
                 .rearrange("p g n t -> p (g n t)")
                 .bitcast(F32)
                 .rearrange("p (g n u) -> p g n u", g=PASSES, u=2),
-                in_=turned[:].rearrange("p (g u) n -> p g n u", u=2),
+                in_=turned_of[nt][:].rearrange("p (g u) n -> p g n u", u=2),
             )
 
-        def add(grp, g):
+        def senders_of(grp, g):
             first = (grp % 2) * GROUP_NODES
-            senders = send_of[grp // 2][:, g, first : first + GROUP_NODES, :].rearrange(
+            return send_of[grp // 2][:, g, first : first + GROUP_NODES, :].rearrange(
                 "p (b j) t -> p b j t", b=GROUP
             )
-            pre = deep.tile([P, GROUP_PAIRS * PACK], BF16, name="pre")
-            pre_of[(grp, g)] = pre
-            pairs = pre[:].rearrange("p (b i j t) -> p b i j t", b=GROUP, i=NODES, j=NODES)
+
+        def pairs_of(grp, g):
+            return pre_of[(grp, g)][:].rearrange(
+                "p (b i j t) -> p b i j t", b=GROUP, i=NODES, j=NODES
+            )
+
+        def pool_add(grp, g):
+            pre_of[(grp, g)] = deep.tile([P, GROUP_PAIRS * PACK], BF16, name="pre")
             shape = [P, POOL_GRAPHS, NODES, NODES, PACK]
             nc.gpsimd.tensor_tensor(
-                out=pairs[:, VECTOR_GRAPHS:GROUP],
+                out=pairs_of(grp, g)[:, VECTOR_GRAPHS:GROUP],
                 in0=recv_copy_of[grp][:, g, :, :]
                 .rearrange("p (b i) t -> p b i t", b=POOL_GRAPHS)
                 .unsqueeze(3)
                 .broadcast_to(shape),
-                in1=senders[:, VECTOR_GRAPHS:GROUP].unsqueeze(2).broadcast_to(shape),
+                in1=senders_of(grp, g)[:, VECTOR_GRAPHS:GROUP].unsqueeze(2).broadcast_to(shape),
                 op=ALU.add,
             )
+
+        def vector_add(grp, g):
             shape = [P, VECTOR_GRAPHS, NODES, NODES, PACK]
             nc.vector.tensor_tensor(
-                out=pairs[:, 0:VECTOR_GRAPHS],
+                out=pairs_of(grp, g)[:, 0:VECTOR_GRAPHS],
                 in0=recv_of[grp][:, PACK * g : PACK * (g + 1), 0:VECTOR_NODES]
                 .rearrange("p t (b i) -> p b i t", b=VECTOR_GRAPHS)
                 .unsqueeze(3)
                 .broadcast_to(shape),
-                in1=senders[:, 0:VECTOR_GRAPHS].unsqueeze(2).broadcast_to(shape),
+                in1=senders_of(grp, g)[:, 0:VECTOR_GRAPHS].unsqueeze(2).broadcast_to(shape),
                 op=ALU.add,
             )
 
@@ -311,28 +326,41 @@ def tile_graphdynamics_pa_t_kernel(
             nc.scalar.copy(out=result[:], in_=turned_out[:])
             nc.sync.dma_start(out=out_rows[nt * NODE_TILE : (nt + 1) * NODE_TILE, :], in_=result[:])
 
-        prepare_receivers(0)
-        prepare_senders(0)
-        for step in range(N_GROUPS + 1):
+        def ahead_of_vector(grp):
+            copy_receivers(grp)
+            if grp % 2 == 0:
+                copy_senders(grp // 2)
+            for g in range(PASSES):
+                pool_add(grp, g)
+
+        def prepare(grp):
+            prepare_receivers(grp)
+            if grp % 2 == 0:
+                turn_senders(grp // 2)
+
+        prepare(0)
+        prepare(1)
+        ahead_of_vector(0)
+        for step in range(N_GROUPS + 2):
+            if 2 <= step:
+                sum_senders(step - 2)
             if step + 1 < N_GROUPS:
-                prepare_receivers(step + 1)
-                if (step + 1) % 2 == 0:
-                    prepare_senders((step + 1) // 2)
+                ahead_of_vector(step + 1)
             if step < N_GROUPS:
-                add(step, 0)
+                vector_add(step, 0)
                 relu(step, 0)
-            if step >= 3 and step % 2 == 1:
-                finish((step - 3) // 2)
-            if step >= 1:
+            if 1 <= step <= N_GROUPS:
                 quantise(step - 1, 1)
                 multiply(step - 1)
             if step < N_GROUPS:
-                add(step, 1)
+                vector_add(step, 1)
                 relu(step, 1)
                 quantise(step, 0)
             if step == 0:
                 build_selection()
-            if step >= 1:
+            if 1 <= step <= N_GROUPS:
                 leave_psum(step - 1)
-                sum_senders(step - 1)
-        finish(N_NODE_TILES - 1)
+            if step + 2 < N_GROUPS:
+                prepare(step + 2)
+            if step >= 3 and step % 2 == 1:
+                finish((step - 3) // 2)

@@ -57,6 +57,7 @@ def tile_graphdynamics_pa_t_kernel(
         keep = stack.enter_context(tc.tile_pool(name="keep", bufs=1))
         work = stack.enter_context(tc.tile_pool(name="work", bufs=2))
         deep = stack.enter_context(tc.tile_pool(name="deep", bufs=4))
+        ring = stack.enter_context(tc.tile_pool(name="ring", bufs=3))
         ps_recv = stack.enter_context(tc.psum_pool(name="ps_recv", bufs=2))
         ps_send = stack.enter_context(tc.psum_pool(name="ps_send", bufs=1))
         ps_acc = stack.enter_context(tc.psum_pool(name="ps_acc", bufs=2))
@@ -84,7 +85,6 @@ def tile_graphdynamics_pa_t_kernel(
         recv_copy_of = {}
         turned_of = {}
         send_of = {}
-        pre_of = {}
         h_of = {}
         codes_of = {}
         scales_of = {}
@@ -191,12 +191,12 @@ def tile_graphdynamics_pa_t_kernel(
             )
 
         def pairs_of(grp, g):
-            return pre_of[(grp, g)][:].rearrange(
+            return h_of[(grp, g)][:].rearrange(
                 "p (b i j t) -> p b i j t", b=GROUP, i=NODES, j=NODES
             )
 
         def pool_add(grp, g):
-            pre_of[(grp, g)] = deep.tile([P, GROUP_PAIRS * PACK], BF16, name="pre")
+            h_of[(grp, g)] = ring.tile([P, GROUP_PAIRS * PACK], BF16, name="h", align_bytes=64)
             shape = [P, POOL_GRAPHS, NODES, NODES, PACK]
             nc.gpsimd.tensor_tensor(
                 out=pairs_of(grp, g)[:, VECTOR_GRAPHS:GROUP],
@@ -221,9 +221,7 @@ def tile_graphdynamics_pa_t_kernel(
             )
 
         def relu(grp, g):
-            h = work.tile([P, GROUP_PAIRS * PACK], BF16, name="h", align_bytes=64)
-            h_of[(grp, g)] = h
-            nc.scalar.activation(out=h[:], in_=pre_of[(grp, g)][:], func=ACT.Relu)
+            nc.scalar.activation(out=h_of[(grp, g)][:], in_=h_of[(grp, g)][:], func=ACT.Relu)
 
         def quantise(grp, g):
             codes = deep.tile([P, GROUP_PAIRS], U32, name="codes", align_bytes=64)

@@ -37,10 +37,13 @@ NODE_TILE = P
 TILE_GRAPHS = NODE_TILE // NODES
 N_NODE_TILES = GRAPHS * NODES // NODE_TILE
 XI_SLOTS = 4
-POOL_GRAPHS = 1
-POOL_NODES = POOL_GRAPHS * NODES
-VECTOR_GRAPHS = GROUP - POOL_GRAPHS
-VECTOR_NODES = VECTOR_GRAPHS * NODES
+POOL_RECEIVERS = 6
+VECTOR_RECEIVERS = NODES - POOL_RECEIVERS
+POOL_COLS = GROUP * POOL_RECEIVERS
+VECTOR_COLS = GROUP * VECTOR_RECEIVERS
+UNITS = N_GROUPS * PASSES
+BANKS = N_GROUPS * PAIR_TILES // BANK_TILES
+NODE_BANKS = BANKS // N_NODE_TILES
 
 FLOPS = 2 * GRAPHS * NODES * NODES * HIDDEN * OUT_DIM
 
@@ -133,7 +136,15 @@ def tile_graphdynamics_pa_t_kernel(
 
         make_identity(nc, ident_bf[:])
         make_identity(nc, ident_f32[:])
-        nc.vector.tensor_copy(out=pick[:], in_=ident_bf[:, 0:GROUP_NODES])
+        by_graph = ident_bf[:, 0:GROUP_NODES].rearrange("p (b i) -> p b i", b=GROUP)
+        nc.vector.tensor_copy(
+            out=pick[:, 0:VECTOR_COLS].rearrange("p (b i) -> p b i", b=GROUP),
+            in_=by_graph[:, :, 0:VECTOR_RECEIVERS],
+        )
+        nc.vector.tensor_copy(
+            out=pick[:, VECTOR_COLS:GROUP_NODES].rearrange("p (b i) -> p b i", b=GROUP),
+            in_=by_graph[:, :, VECTOR_RECEIVERS:NODES],
+        )
         nc.vector.memset(pick[GROUP_NODES : GROUP_NODES + 1, :], 1.0)
 
         def prepare_receivers(grp):
@@ -152,11 +163,11 @@ def tile_graphdynamics_pa_t_kernel(
                 load_receivers(grp + XI_SLOTS)
 
         def copy_receivers(grp):
-            recv_copy = work.tile([P, PASSES, POOL_NODES, PACK], F32, name="recv_copy")
+            recv_copy = work.tile([P, PASSES, POOL_COLS, PACK], F32, name="recv_copy")
             recv_copy_of[grp] = recv_copy
             nc.scalar.copy(
                 out=recv_copy[:],
-                in_=recv_of[grp][:, :, VECTOR_NODES:GROUP_NODES].rearrange(
+                in_=recv_of[grp][:, :, VECTOR_COLS:GROUP_NODES].rearrange(
                     "p (g t) n -> p g n t", t=PACK
                 ),
             )
@@ -197,31 +208,35 @@ def tile_graphdynamics_pa_t_kernel(
 
         def pool_add(grp, g):
             h_of[(grp, g)] = ring.tile([P, GROUP_PAIRS * PACK], BF16, name="h", align_bytes=64)
-            shape = [P, POOL_GRAPHS, NODES, NODES, PACK]
+            shape = [P, GROUP, POOL_RECEIVERS, NODES, PACK]
             nc.gpsimd.tensor_tensor(
-                out=pairs_of(grp, g)[:, VECTOR_GRAPHS:GROUP],
+                out=pairs_of(grp, g)[:, :, VECTOR_RECEIVERS:NODES],
                 in0=recv_copy_of[grp][:, g, :, :]
-                .rearrange("p (b i) t -> p b i t", b=POOL_GRAPHS)
+                .rearrange("p (b i) t -> p b i t", b=GROUP)
                 .unsqueeze(3)
                 .broadcast_to(shape),
-                in1=senders_of(grp, g)[:, VECTOR_GRAPHS:GROUP].unsqueeze(2).broadcast_to(shape),
+                in1=senders_of(grp, g).unsqueeze(2).broadcast_to(shape),
                 op=ALU.add,
             )
 
         def vector_add(grp, g):
-            shape = [P, VECTOR_GRAPHS, NODES, NODES, PACK]
+            shape = [P, GROUP, VECTOR_RECEIVERS, NODES, PACK]
             nc.vector.tensor_tensor(
-                out=pairs_of(grp, g)[:, 0:VECTOR_GRAPHS],
-                in0=recv_of[grp][:, PACK * g : PACK * (g + 1), 0:VECTOR_NODES]
-                .rearrange("p t (b i) -> p b i t", b=VECTOR_GRAPHS)
+                out=pairs_of(grp, g)[:, :, 0:VECTOR_RECEIVERS],
+                in0=recv_of[grp][:, PACK * g : PACK * (g + 1), 0:VECTOR_COLS]
+                .rearrange("p t (b i) -> p b i t", b=GROUP)
                 .unsqueeze(3)
                 .broadcast_to(shape),
-                in1=senders_of(grp, g)[:, 0:VECTOR_GRAPHS].unsqueeze(2).broadcast_to(shape),
+                in1=senders_of(grp, g).unsqueeze(2).broadcast_to(shape),
                 op=ALU.add,
             )
 
         def relu(grp, g):
-            nc.scalar.activation(out=h_of[(grp, g)][:], in_=h_of[(grp, g)][:], func=ACT.Relu)
+            h = h_of[(grp, g)]
+            if (grp, g) == (N_GROUPS - 1, PASSES - 1):
+                nc.vector.tensor_scalar_max(out=h[:], in0=h[:], scalar1=0.0)
+            else:
+                nc.scalar.activation(out=h[:], in_=h[:], func=ACT.Relu)
 
         def quantise(grp, g):
             codes = deep.tile([P, GROUP_PAIRS], U32, name="codes", align_bytes=64)
@@ -233,7 +248,7 @@ def tile_graphdynamics_pa_t_kernel(
         def multiply(grp):
             for bank in range(PAIR_TILES // BANK_TILES):
                 acc = ps_acc.tile([P, BANK_TILES, OUT_DIM], F32, name="acc")
-                acc_of[(grp, bank)] = acc
+                acc_of[grp * (PAIR_TILES // BANK_TILES) + bank] = acc
                 for c in range(BANK_TILES):
                     first = (bank * BANK_TILES + c) * PAIR_TILE
                     for g in range(PASSES):
@@ -247,28 +262,27 @@ def tile_graphdynamics_pa_t_kernel(
                             stop=(g == PASSES - 1),
                         )
 
-        def leave_psum(grp):
-            for bank in range(PAIR_TILES // BANK_TILES):
-                floored = deep.tile([P, BANK_TILES, OUT_DIM], F32, name="floored")
-                floor_of[(grp, bank)] = floored
-                nc.vector.tensor_tensor(
-                    out=floored[:],
-                    in0=acc_of[(grp, bank)][:],
-                    in1=neg_bias[:].unsqueeze(1).broadcast_to([P, BANK_TILES, OUT_DIM]),
-                    op=ALU.max,
-                )
+        def leave_psum(bank):
+            floored = deep.tile([P, BANK_TILES, OUT_DIM], F32, name="floored")
+            floor_of[bank] = floored
+            nc.vector.tensor_tensor(
+                out=floored[:],
+                in0=acc_of[bank][:],
+                in1=neg_bias[:].unsqueeze(1).broadcast_to([P, BANK_TILES, OUT_DIM]),
+                op=ALU.max,
+            )
 
-        def sum_senders(grp):
-            nt = grp // 2
-            if grp % 2 == 0:
+        def sum_senders(bank):
+            nt, place = divmod(bank, NODE_BANKS)
+            if place == 0:
                 sums_of[nt] = ps_sum.tile([P, NODE_TILE], F32, name="sums")
-            for tile in range(PAIR_TILES):
-                bank, c = divmod(tile, BANK_TILES)
-                first = ((grp % 2) * PAIR_TILES + tile) * TILE_RECEIVERS
+            for c in range(BANK_TILES):
+                tile = bank * BANK_TILES + c
+                first = (place * BANK_TILES + c) * TILE_RECEIVERS
                 nc.tensor.matmul(
                     out=sums_of[nt][:, first : first + TILE_RECEIVERS],
-                    lhsT=floor_of[(grp, bank)][:, c, :],
-                    rhs=sel[:, grp * GROUP + tile // 2, :],
+                    lhsT=floor_of[bank][:, c, :],
+                    rhs=sel[:, tile // 2, :],
                     start=True,
                     stop=True,
                 )
@@ -324,41 +338,39 @@ def tile_graphdynamics_pa_t_kernel(
             nc.scalar.copy(out=result[:], in_=turned_out[:])
             nc.sync.dma_start(out=out_rows[nt * NODE_TILE : (nt + 1) * NODE_TILE, :], in_=result[:])
 
-        def ahead_of_vector(grp):
-            copy_receivers(grp)
-            if grp % 2 == 0:
-                copy_senders(grp // 2)
-            for g in range(PASSES):
-                pool_add(grp, g)
-
         def prepare(grp):
             prepare_receivers(grp)
             if grp % 2 == 0:
                 turn_senders(grp // 2)
 
+        def ahead_of_vector(unit):
+            grp, g = divmod(unit, PASSES)
+            if g == 0:
+                copy_receivers(grp)
+                if grp % 2 == 0:
+                    copy_senders(grp // 2)
+            pool_add(grp, g)
+
         prepare(0)
         prepare(1)
         ahead_of_vector(0)
-        for step in range(N_GROUPS + 2):
-            if 2 <= step:
-                sum_senders(step - 2)
-            if step + 1 < N_GROUPS:
-                ahead_of_vector(step + 1)
-            if step < N_GROUPS:
-                vector_add(step, 0)
-                relu(step, 0)
-            if 1 <= step <= N_GROUPS:
-                quantise(step - 1, 1)
-                multiply(step - 1)
-            if step < N_GROUPS:
-                vector_add(step, 1)
-                relu(step, 1)
-                quantise(step, 0)
-            if step == 0:
+        ahead_of_vector(1)
+        for u in range(UNITS + 4):
+            if u + 2 < UNITS:
+                ahead_of_vector(u + 2)
+            if u < UNITS:
+                vector_add(u // PASSES, u % PASSES)
+                relu(u // PASSES, u % PASSES)
+            if u % PASSES == 1 and (u + 3) // PASSES < N_GROUPS:
+                prepare((u + 3) // PASSES)
+            if 1 <= u <= UNITS:
+                quantise((u - 1) // PASSES, (u - 1) % PASSES)
+                if u % PASSES == 0:
+                    multiply(u // PASSES - 1)
+            if u == 1:
                 build_selection()
-            if 1 <= step <= N_GROUPS:
-                leave_psum(step - 1)
-            if step + 2 < N_GROUPS:
-                prepare(step + 2)
-            if step >= 3 and step % 2 == 1:
-                finish((step - 3) // 2)
+            if 3 <= u < BANKS + 3:
+                leave_psum(u - 3)
+                sum_senders(u - 3)
+            if u >= NODE_BANKS + 3 and (u - 3) % NODE_BANKS == 0:
+                finish((u - 3) // NODE_BANKS - 1)

@@ -60,7 +60,7 @@ def tile_graphdynamics_pa_t_kernel(
         keep = stack.enter_context(tc.tile_pool(name="keep", bufs=1))
         work = stack.enter_context(tc.tile_pool(name="work", bufs=2))
         deep = stack.enter_context(tc.tile_pool(name="deep", bufs=4))
-        ring = stack.enter_context(tc.tile_pool(name="ring", bufs=3))
+        ring = stack.enter_context(tc.tile_pool(name="ring", bufs=4))
         ps_recv = stack.enter_context(tc.psum_pool(name="ps_recv", bufs=2))
         ps_send = stack.enter_context(tc.psum_pool(name="ps_send", bufs=1))
         ps_acc = stack.enter_context(tc.psum_pool(name="ps_acc", bufs=2))
@@ -310,6 +310,8 @@ def tile_graphdynamics_pa_t_kernel(
                 in1=same_receiver[:].unsqueeze(1).broadcast_to([P, GRAPHS, TILE_RECEIVERS]),
                 op=ALU.mult,
             )
+
+        def build_bias_share():
             share = ps_misc.tile([P, GRAPHS * TILE_RECEIVERS], F32, name="share", tag="misc")
             nc.tensor.matmul(
                 out=share[:],
@@ -351,11 +353,12 @@ def tile_graphdynamics_pa_t_kernel(
                     copy_senders(grp // 2)
             pool_add(grp, g)
 
+        build_selection()
         prepare(0)
         prepare(1)
         ahead_of_vector(0)
         ahead_of_vector(1)
-        for u in range(UNITS + 4):
+        for u in range(UNITS + 5):
             if u + 2 < UNITS:
                 ahead_of_vector(u + 2)
             if u < UNITS:
@@ -363,14 +366,14 @@ def tile_graphdynamics_pa_t_kernel(
                 relu(u // PASSES, u % PASSES)
             if u % PASSES == 1 and (u + 3) // PASSES < N_GROUPS:
                 prepare((u + 3) // PASSES)
-            if 1 <= u <= UNITS:
-                quantise((u - 1) // PASSES, (u - 1) % PASSES)
-                if u % PASSES == 0:
-                    multiply(u // PASSES - 1)
+            if 2 <= u < UNITS + 2:
+                quantise((u - 2) // PASSES, (u - 2) % PASSES)
+                if u % PASSES == 1:
+                    multiply((u - 2) // PASSES)
             if u == 1:
-                build_selection()
-            if 3 <= u < BANKS + 3:
-                leave_psum(u - 3)
-                sum_senders(u - 3)
-            if u >= NODE_BANKS + 3 and (u - 3) % NODE_BANKS == 0:
-                finish((u - 3) // NODE_BANKS - 1)
+                build_bias_share()
+            if 4 <= u < BANKS + 4:
+                leave_psum(u - 4)
+                sum_senders(u - 4)
+            if u >= NODE_BANKS + 4 and (u - 4) % NODE_BANKS == 0:
+                finish((u - 4) // NODE_BANKS - 1)

@@ -37,6 +37,7 @@ NODE_TILE = P
 TILE_GRAPHS = NODE_TILE // NODES
 N_NODE_TILES = GRAPHS * NODES // NODE_TILE
 XI_SLOTS = 4
+BIAS_ROWS_END = 96
 POOL_RECEIVERS = 6
 VECTOR_RECEIVERS = NODES - POOL_RECEIVERS
 POOL_COLS = GROUP * POOL_RECEIVERS
@@ -106,16 +107,21 @@ def tile_graphdynamics_pa_t_kernel(
                 out=xj_sb[:, nt, :], in_=xj_rows[nt * NODE_TILE : (nt + 1) * NODE_TILE, :]
             )
 
-        nc.vector.memset(xi_aug[GROUP_NODES:P, :, :].bitcast(I32), 0)
-        nc.vector.memset(w_scales[:].bitcast(I32), 0)
-        nc.vector.memset(mask_rows[:], 0.0)
-
         nc.scalar.dma_start(
-            out=xi_aug[GROUP_NODES : GROUP_NODES + 1, :, :],
-            in_=mb1.unsqueeze(0).unsqueeze(0).broadcast_to([1, XI_SLOTS, HIDDEN]),
+            out=xi_aug[GROUP_NODES:BIAS_ROWS_END, 0:1, :],
+            in_=mb1.unsqueeze(0).unsqueeze(0).broadcast_to([BIAS_ROWS_END - GROUP_NODES, 1, HIDDEN]),
         )
+        nc.vector.memset(mask_rows[:], 0.0)
+        nc.vector.memset(xi_aug[BIAS_ROWS_END:P, 0:1, :].bitcast(I32), 0)
+        nc.vector.memset(w_scales[:].bitcast(I32), 0)
+        nc.vector.memset(xi_aug[GROUP_NODES:P, 1:XI_SLOTS, :].bitcast(I32), 0)
+
         nc.scalar.dma_start(out=bias_bf[:], in_=mb2.partition_broadcast(P))
         nc.scalar.dma_start(out=mask_rows[0:GRAPHS, :], in_=node_mask)
+        nc.scalar.dma_start(
+            out=xi_aug[GROUP_NODES : GROUP_NODES + 1, 1:XI_SLOTS, :],
+            in_=mb1.unsqueeze(0).unsqueeze(0).broadcast_to([1, XI_SLOTS - 1, HIDDEN]),
+        )
 
         load_receivers(0)
         load_senders(0)
@@ -348,15 +354,15 @@ def tile_graphdynamics_pa_t_kernel(
         def ahead_of_vector(unit):
             grp, g = divmod(unit, PASSES)
             if g == 0:
-                copy_receivers(grp)
                 if grp % 2 == 0:
                     copy_senders(grp // 2)
+                copy_receivers(grp)
             pool_add(grp, g)
 
-        build_selection()
         prepare(0)
-        prepare(1)
         ahead_of_vector(0)
+        build_selection()
+        prepare(1)
         ahead_of_vector(1)
         for u in range(UNITS + 5):
             if u + 2 < UNITS:

@@ -42,6 +42,7 @@ POOL_RECEIVERS = 6
 VECTOR_RECEIVERS = NODES - POOL_RECEIVERS
 POOL_COLS = GROUP * POOL_RECEIVERS
 VECTOR_COLS = GROUP * VECTOR_RECEIVERS
+VECTOR_RELU_EVERY = 16
 UNITS = N_GROUPS * PASSES
 BANKS = N_GROUPS * PAIR_TILES // BANK_TILES
 NODE_BANKS = BANKS // N_NODE_TILES
@@ -237,9 +238,12 @@ def tile_graphdynamics_pa_t_kernel(
                 op=ALU.add,
             )
 
+        def on_vector(unit):
+            return unit % VECTOR_RELU_EVERY == VECTOR_RELU_EVERY - 1
+
         def relu(grp, g):
             h = h_of[(grp, g)]
-            if (grp, g) == (N_GROUPS - 1, PASSES - 1):
+            if on_vector(grp * PASSES + g):
                 nc.vector.tensor_scalar_max(out=h[:], in0=h[:], scalar1=0.0)
             else:
                 nc.scalar.activation(out=h[:], in_=h[:], func=ACT.Relu)
@@ -369,9 +373,12 @@ def tile_graphdynamics_pa_t_kernel(
                 ahead_of_vector(u + 2)
             if u < UNITS:
                 vector_add(u // PASSES, u % PASSES)
-                relu(u // PASSES, u % PASSES)
+                if not on_vector(u):
+                    relu(u // PASSES, u % PASSES)
             if u % PASSES == 1 and (u + 3) // PASSES < N_GROUPS:
                 prepare((u + 3) // PASSES)
+            if 1 <= u <= UNITS and on_vector(u - 1):
+                relu((u - 1) // PASSES, (u - 1) % PASSES)
             if 2 <= u < UNITS + 2:
                 quantise((u - 2) // PASSES, (u - 2) % PASSES)
                 if u % PASSES == 1:

@@ -355,6 +355,10 @@ def tile_graphdynamics_pa_t_kernel(
             if grp % 2 == 0:
                 turn_senders(grp // 2)
 
+        def empty_bank(bank):
+            leave_psum(bank)
+            sum_senders(bank)
+
         def ahead_of_vector(unit):
             grp, g = divmod(unit, PASSES)
             if g == 0:
@@ -368,7 +372,7 @@ def tile_graphdynamics_pa_t_kernel(
         build_selection()
         prepare(1)
         ahead_of_vector(1)
-        for u in range(UNITS + 5):
+        for u in range(UNITS - 1):
             if u + 2 < UNITS:
                 ahead_of_vector(u + 2)
             if u < UNITS:
@@ -390,3 +394,18 @@ def tile_graphdynamics_pa_t_kernel(
                 sum_senders(u - 4)
             if u >= NODE_BANKS + 4 and (u - 4) % NODE_BANKS == 0:
                 finish((u - 4) // NODE_BANKS - 1)
+        last = N_GROUPS - 1
+        empty_bank(BANKS - 5)
+        quantise(last - 1, 1)
+        multiply(last - 1)
+        vector_add(last, 1)
+        empty_bank(BANKS - 4)
+        relu(last, 1)
+        empty_bank(BANKS - 3)
+        quantise(last, 0)
+        quantise(last, 1)
+        multiply(last)
+        finish(N_NODE_TILES - 2)
+        empty_bank(BANKS - 2)
+        empty_bank(BANKS - 1)
+        finish(N_NODE_TILES - 1)

@@ -29,23 +29,25 @@ GROUP = 4
 GROUP_NODES = GROUP * NODES
 GROUP_PAIRS = GROUP * NODES * NODES
 N_GROUPS = GRAPHS // GROUP
-PAIR_TILE = P
-TILE_RECEIVERS = PAIR_TILE // NODES
-PAIR_TILES = GROUP_PAIRS // PAIR_TILE
-BANK_TILES = 4
+BANK_PAIRS = 512
+GROUP_BANKS = GROUP_PAIRS // BANK_PAIRS
+BANK_ROWS = BANK_PAIRS // NODES
 NODE_TILE = P
 TILE_GRAPHS = NODE_TILE // NODES
 N_NODE_TILES = GRAPHS * NODES // NODE_TILE
+NODE_BANKS = NODE_TILE // BANK_ROWS
+BANKS = N_GROUPS * GROUP_BANKS
+TILE_RECEIVERS = P // NODES
+MASK_STEP = 16
 XI_SLOTS = 4
 BIAS_ROWS_END = 96
-POOL_RECEIVERS = 6
+POOL_RECEIVERS = 5
 VECTOR_RECEIVERS = NODES - POOL_RECEIVERS
 POOL_COLS = GROUP * POOL_RECEIVERS
 VECTOR_COLS = GROUP * VECTOR_RECEIVERS
-VECTOR_RELU_EVERY = 16
+VECTOR_RELU_EVERY = 5
 UNITS = N_GROUPS * PASSES
-BANKS = N_GROUPS * PAIR_TILES // BANK_TILES
-NODE_BANKS = BANKS // N_NODE_TILES
+FAR_BELOW = -3.0e38
 
 FLOPS = 2 * GRAPHS * NODES * NODES * HIDDEN * OUT_DIM
 
@@ -63,10 +65,9 @@ def tile_graphdynamics_pa_t_kernel(
         work = stack.enter_context(tc.tile_pool(name="work", bufs=2))
         deep = stack.enter_context(tc.tile_pool(name="deep", bufs=4))
         ring = stack.enter_context(tc.tile_pool(name="ring", bufs=4))
-        ps_recv = stack.enter_context(tc.psum_pool(name="ps_recv", bufs=2))
+        ps_recv = stack.enter_context(tc.psum_pool(name="ps_recv", bufs=3))
         ps_send = stack.enter_context(tc.psum_pool(name="ps_send", bufs=1))
-        ps_acc = stack.enter_context(tc.psum_pool(name="ps_acc", bufs=2))
-        ps_sum = stack.enter_context(tc.psum_pool(name="ps_sum", bufs=2))
+        ps_acc = stack.enter_context(tc.psum_pool(name="ps_acc", bufs=3))
         ps_misc = stack.enter_context(tc.psum_pool(name="ps_misc", bufs=1))
         stack.enter_context(tc.manual_schedule())
 
@@ -79,12 +80,17 @@ def tile_graphdynamics_pa_t_kernel(
         w_scales = keep.tile([P, PASSES, OUT_DIM], U8, name="w_scales", align_bytes=64)
         mask_rows = keep.tile([P, NODES], BF16, name="mask_rows")
         mask_wide = keep.tile([P, TILE_RECEIVERS, NODES], BF16, name="mask_wide")
+        mask_col = keep.tile([P, N_NODE_TILES, MASK_STEP], BF16, name="mask_col")
+        keep_col = keep.tile([P, N_NODE_TILES], F32, name="keep_col")
+        drop_col = keep.tile([P, N_NODE_TILES], F32, name="drop_col")
         bias_bf = keep.tile([P, OUT_DIM], BF16, name="bias_bf")
-        bias_rows = keep.tile([P, OUT_DIM], F32, name="bias_rows")
-        neg_bias = keep.tile([P, OUT_DIM], F32, name="neg_bias")
+        relu_rows = keep.tile([P, OUT_DIM], F32, name="relu_rows")
+        bias_pair = keep.tile([P, 2], BF16, name="bias_pair")
+        bias_col = keep.tile([P, 1], F32, name="bias_col")
+        all_padded = keep.tile([P, 1], F32, name="all_padded")
         same_receiver = keep.tile([P, TILE_RECEIVERS], F32, name="same_receiver")
         sel = keep.tile([P, GRAPHS, TILE_RECEIVERS], F32, name="sel")
-        bias_share = keep.tile([P, GRAPHS, TILE_RECEIVERS], F32, name="bias_share")
+        surplus = keep.tile([P, GRAPHS, NODES // TILE_RECEIVERS, TILE_RECEIVERS], F32, name="surplus")
 
         recv_of = {}
         recv_copy_of = {}
@@ -94,8 +100,8 @@ def tile_graphdynamics_pa_t_kernel(
         codes_of = {}
         scales_of = {}
         acc_of = {}
-        floor_of = {}
-        sums_of = {}
+        msgs_of = {}
+        total_of = {}
 
         def load_receivers(grp):
             nc.sync.dma_start(
@@ -108,10 +114,18 @@ def tile_graphdynamics_pa_t_kernel(
                 out=xj_sb[:, nt, :], in_=xj_rows[nt * NODE_TILE : (nt + 1) * NODE_TILE, :]
             )
 
+        def load_mask_columns(first, end):
+            nc.scalar.dma_start(
+                out=mask_col[:, first:end, 0:1],
+                in_=node_mask.rearrange("(n b) j -> (b j) n", b=TILE_GRAPHS)[:, first:end].unsqueeze(2),
+            )
+
         nc.scalar.dma_start(
             out=xi_aug[GROUP_NODES:BIAS_ROWS_END, 0:1, :],
             in_=mb1.unsqueeze(0).unsqueeze(0).broadcast_to([BIAS_ROWS_END - GROUP_NODES, 1, HIDDEN]),
         )
+        stack.enter_context(nc.allow_non_contiguous_dma(reason="one mask or bias value to a partition"))
+        load_mask_columns(0, 1)
         nc.vector.memset(mask_rows[:], 0.0)
         nc.vector.memset(xi_aug[BIAS_ROWS_END:P, 0:1, :].bitcast(I32), 0)
         nc.vector.memset(w_scales[:].bitcast(I32), 0)
@@ -123,6 +137,8 @@ def tile_graphdynamics_pa_t_kernel(
             out=xi_aug[GROUP_NODES : GROUP_NODES + 1, 1:XI_SLOTS, :],
             in_=mb1.unsqueeze(0).unsqueeze(0).broadcast_to([1, XI_SLOTS - 1, HIDDEN]),
         )
+        load_mask_columns(1, N_NODE_TILES)
+        nc.scalar.dma_start(out=bias_pair[:, 0:1], in_=mb2.rearrange("(d o) -> d o", o=1))
 
         load_receivers(0)
         load_senders(0)
@@ -154,6 +170,27 @@ def tile_graphdynamics_pa_t_kernel(
         )
         nc.vector.memset(pick[GROUP_NODES : GROUP_NODES + 1, :], 1.0)
 
+        def mask_factors(first, end):
+            nc.vector.tensor_copy(out=keep_col[:, first:end], in_=mask_col[:, first:end, 0])
+            nc.vector.tensor_scalar(
+                out=drop_col[:, first:end],
+                in0=mask_col[:, first:end, 0],
+                scalar1=-1.0,
+                scalar2=-FAR_BELOW,
+                op0=ALU.add,
+                op1=ALU.mult,
+            )
+
+        def mask_senders(nt):
+            nc.vector.tensor_scalar(
+                out=xj_sb[:, nt, :],
+                in0=xj_sb[:, nt, :],
+                scalar1=keep_col[:, nt : nt + 1],
+                scalar2=drop_col[:, nt : nt + 1],
+                op0=ALU.mult,
+                op1=ALU.add,
+            )
+
         def prepare_receivers(grp):
             recv = ps_recv.tile([P, PLANES, GROUP_NODES], F32, name="recv")
             recv_of[grp] = recv
@@ -170,7 +207,7 @@ def tile_graphdynamics_pa_t_kernel(
                 load_receivers(grp + XI_SLOTS)
 
         def copy_receivers(grp):
-            recv_copy = work.tile([P, PASSES, POOL_COLS, PACK], F32, name="recv_copy")
+            recv_copy = deep.tile([P, PASSES, POOL_COLS, PACK], F32, name="recv_copy")
             recv_copy_of[grp] = recv_copy
             nc.scalar.copy(
                 out=recv_copy[:],
@@ -239,7 +276,7 @@ def tile_graphdynamics_pa_t_kernel(
             )
 
         def on_vector(unit):
-            return unit % VECTOR_RELU_EVERY == VECTOR_RELU_EVERY - 1
+            return unit % VECTOR_RELU_EVERY == VECTOR_RELU_EVERY - 1 or unit == UNITS - 1
 
         def relu(grp, g):
             h = h_of[(grp, g)]
@@ -255,51 +292,65 @@ def tile_graphdynamics_pa_t_kernel(
             scales_of[(grp, g)] = scales
             nc.vector.quantize_mx(out=codes[:].bitcast(FP8X4), scales=scales[:], in_=h_of[(grp, g)][:])
 
-        def multiply(grp):
-            for bank in range(PAIR_TILES // BANK_TILES):
-                acc = ps_acc.tile([P, BANK_TILES, OUT_DIM], F32, name="acc")
-                acc_of[grp * (PAIR_TILES // BANK_TILES) + bank] = acc
-                for c in range(BANK_TILES):
-                    first = (bank * BANK_TILES + c) * PAIR_TILE
-                    for g in range(PASSES):
-                        nc.tensor.matmul_mx(
-                            out=acc[:, c, :],
-                            lhsT=codes_of[(grp, g)][:, first : first + PAIR_TILE].bitcast(FP8X4),
-                            lhsT_scale=scales_of[(grp, g)][:, first : first + PAIR_TILE],
-                            rhs=w_words[:, g, :].bitcast(FP4X4),
-                            rhs_scale=w_scales[:, g, :],
-                            start=(g == 0),
-                            stop=(g == PASSES - 1),
-                        )
-
-        def leave_psum(bank):
-            floored = deep.tile([P, BANK_TILES, OUT_DIM], F32, name="floored")
-            floor_of[bank] = floored
-            nc.vector.tensor_tensor(
-                out=floored[:],
-                in0=acc_of[bank][:],
-                in1=neg_bias[:].unsqueeze(1).broadcast_to([P, BANK_TILES, OUT_DIM]),
-                op=ALU.max,
-            )
-
-        def sum_senders(bank):
-            nt, place = divmod(bank, NODE_BANKS)
-            if place == 0:
-                sums_of[nt] = ps_sum.tile([P, NODE_TILE], F32, name="sums")
-            for c in range(BANK_TILES):
-                tile = bank * BANK_TILES + c
-                first = (place * BANK_TILES + c) * TILE_RECEIVERS
-                nc.tensor.matmul(
-                    out=sums_of[nt][:, first : first + TILE_RECEIVERS],
-                    lhsT=floor_of[bank][:, c, :],
-                    rhs=sel[:, tile // 2, :],
-                    start=True,
-                    stop=True,
+        def multiply(grp, g):
+            for half in range(GROUP_BANKS):
+                bank = grp * GROUP_BANKS + half
+                if g == 0:
+                    acc_of[bank] = ps_acc.tile([P, BANK_PAIRS], F32, name="acc")
+                first = half * BANK_PAIRS
+                nc.tensor.matmul_mx(
+                    out=acc_of[bank][:],
+                    lhsT=w_words[:, g, :].bitcast(FP4X4),
+                    lhsT_scale=w_scales[:, g, :],
+                    rhs=codes_of[(grp, g)][:, first : first + BANK_PAIRS].bitcast(FP8X4),
+                    rhs_scale=scales_of[(grp, g)][:, first : first + BANK_PAIRS],
+                    start=(g == 0),
+                    stop=(g == PASSES - 1),
                 )
 
+        def empty_bank(bank):
+            nt, place = divmod(bank, NODE_BANKS)
+            if place == 0:
+                msgs_of[nt] = work.tile([P, NODES, NODE_TILE], F32, name="msgs")
+            rows = msgs_of[nt][:, :, place * BANK_ROWS : (place + 1) * BANK_ROWS]
+            products = acc_of[bank][:].rearrange("p (r j) -> p j r", j=NODES)
+            if bank == BANKS - 1:
+                nc.vector.tensor_scalar(
+                    out=rows, in0=products, scalar1=bias_col[:, 0:1], scalar2=0.0, op0=ALU.add, op1=ALU.max
+                )
+            else:
+                nc.scalar.activation(out=rows, in_=products, func=ACT.Relu, bias=bias_col[:, 0:1])
+
+        def sum_senders(nt):
+            total = ps_misc.tile([P, OUT_DIM], F32, name="total", tag="misc")
+            total_of[nt] = total
+            nc.tensor.matmul(
+                out=total[:],
+                lhsT=surplus[:, nt * TILE_GRAPHS : (nt + 1) * TILE_GRAPHS, :, :].rearrange(
+                    "p b s i -> p (b s i)"
+                ),
+                rhs=ident_f32[:],
+                start=True,
+                stop=False,
+                is_transpose=True,
+            )
+            for j in range(NODES):
+                nc.tensor.matmul(
+                    out=total[:],
+                    lhsT=msgs_of[nt][:, j, :],
+                    rhs=ident_f32[:],
+                    start=False,
+                    stop=(j == NODES - 1),
+                    is_transpose=True,
+                )
+
+        def finish(nt):
+            result = work.tile([P, OUT_DIM], F32, name="result")
+            nc.scalar.copy(out=result[:], in_=total_of[nt][:])
+            nc.sync.dma_start(out=out_rows[nt * NODE_TILE : (nt + 1) * NODE_TILE, :], in_=result[:])
+
         def build_selection():
-            nc.vector.tensor_copy(out=bias_rows[:], in_=bias_bf[:])
-            nc.vector.tensor_scalar_mul(out=neg_bias[:], in0=bias_bf[:], scalar1=-1.0)
+            nc.vector.tensor_scalar_max(out=relu_rows[:], in0=bias_bf[:], scalar1=0.0)
             nc.vector.tensor_copy(
                 out=mask_wide[:],
                 in_=mask_rows[:].unsqueeze(1).broadcast_to([P, TILE_RECEIVERS, NODES]),
@@ -321,91 +372,78 @@ def tile_graphdynamics_pa_t_kernel(
                 op=ALU.mult,
             )
 
-        def build_bias_share():
+        def build_surplus():
+            nc.vector.tensor_copy(out=bias_col[:], in_=bias_pair[:, 0:1])
+            nc.vector.tensor_scalar(
+                out=all_padded[:],
+                in0=bias_pair[:, 0:1],
+                scalar1=0.0,
+                scalar2=-1.0 * NODES,
+                op0=ALU.max,
+                op1=ALU.mult,
+            )
             share = ps_misc.tile([P, GRAPHS * TILE_RECEIVERS], F32, name="share", tag="misc")
             nc.tensor.matmul(
                 out=share[:],
-                lhsT=bias_rows[:],
+                lhsT=relu_rows[:],
                 rhs=sel[:].rearrange("p b i -> p (b i)"),
                 start=True,
                 stop=True,
             )
-            nc.scalar.copy(out=bias_share[:].rearrange("p b i -> p (b i)"), in_=share[:])
-
-        def finish(nt):
-            halves = NODES // TILE_RECEIVERS
-            shape = [P, TILE_GRAPHS, halves, TILE_RECEIVERS]
-            total = work.tile([P, NODE_TILE], F32, name="total")
-            nc.vector.tensor_tensor(
-                out=total[:].rearrange("p (b s i) -> p b s i", b=TILE_GRAPHS, s=halves),
-                in0=sums_of[nt][:].rearrange("p (b s i) -> p b s i", b=TILE_GRAPHS, s=halves),
-                in1=bias_share[:, nt * TILE_GRAPHS : (nt + 1) * TILE_GRAPHS, :]
+            nc.scalar.activation(
+                out=surplus[:],
+                in_=share[:]
+                .rearrange("p (b i) -> p b i", i=TILE_RECEIVERS)
                 .unsqueeze(2)
-                .broadcast_to(shape),
-                op=ALU.add,
+                .broadcast_to([P, GRAPHS, NODES // TILE_RECEIVERS, TILE_RECEIVERS]),
+                func=ACT.Identity,
+                bias=all_padded[:, 0:1],
             )
-            turned_out = ps_misc.tile([P, OUT_DIM], F32, name="turned_out", tag="misc")
-            nc.tensor.transpose(out=turned_out[:], in_=total[:], identity=ident_f32[:])
-            result = work.tile([P, OUT_DIM], F32, name="result")
-            nc.scalar.copy(out=result[:], in_=turned_out[:])
-            nc.sync.dma_start(out=out_rows[nt * NODE_TILE : (nt + 1) * NODE_TILE, :], in_=result[:])
 
         def prepare(grp):
             prepare_receivers(grp)
             if grp % 2 == 0:
+                mask_senders(grp // 2)
                 turn_senders(grp // 2)
 
-        def empty_bank(bank):
-            leave_psum(bank)
-            sum_senders(bank)
+        def copy_prepared(grp):
+            if grp % 2 == 0:
+                copy_senders(grp // 2)
+            copy_receivers(grp)
 
-        def ahead_of_vector(unit):
-            grp, g = divmod(unit, PASSES)
-            if g == 0:
-                if grp % 2 == 0:
-                    copy_senders(grp // 2)
-                copy_receivers(grp)
-            pool_add(grp, g)
-
+        mask_factors(0, 1)
         prepare(0)
-        ahead_of_vector(0)
+        copy_prepared(0)
+        pool_add(0, 0)
         build_selection()
         prepare(1)
-        ahead_of_vector(1)
-        for u in range(UNITS - 1):
+        copy_prepared(1)
+        pool_add(0, 1)
+        for u in range(UNITS + 4):
             if u + 2 < UNITS:
-                ahead_of_vector(u + 2)
+                pool_add((u + 2) // PASSES, (u + 2) % PASSES)
             if u < UNITS:
                 vector_add(u // PASSES, u % PASSES)
                 if not on_vector(u):
                     relu(u // PASSES, u % PASSES)
-            if u % PASSES == 1 and (u + 3) // PASSES < N_GROUPS:
-                prepare((u + 3) // PASSES)
             if 1 <= u <= UNITS and on_vector(u - 1):
                 relu((u - 1) // PASSES, (u - 1) % PASSES)
+            if u == 0:
+                mask_factors(1, N_NODE_TILES)
+                prepare(2)
+            elif u % PASSES == 1 and (u + 5) // PASSES < N_GROUPS:
+                prepare((u + 5) // PASSES)
             if 2 <= u < UNITS + 2:
                 quantise((u - 2) // PASSES, (u - 2) % PASSES)
-                if u % PASSES == 1:
-                    multiply((u - 2) // PASSES)
+                multiply((u - 2) // PASSES, (u - 2) % PASSES)
             if u == 1:
-                build_bias_share()
-            if 4 <= u < BANKS + 4:
-                leave_psum(u - 4)
-                sum_senders(u - 4)
-            if u >= NODE_BANKS + 4 and (u - 4) % NODE_BANKS == 0:
-                finish((u - 4) // NODE_BANKS - 1)
-        last = N_GROUPS - 1
-        empty_bank(BANKS - 5)
-        quantise(last - 1, 1)
-        multiply(last - 1)
-        vector_add(last, 1)
-        empty_bank(BANKS - 4)
-        relu(last, 1)
-        empty_bank(BANKS - 3)
-        quantise(last, 0)
-        quantise(last, 1)
-        multiply(last)
-        finish(N_NODE_TILES - 2)
-        empty_bank(BANKS - 2)
-        empty_bank(BANKS - 1)
-        finish(N_NODE_TILES - 1)
+                build_surplus()
+                copy_prepared(2)
+            elif u >= 2 and u % PASSES == 0 and (u + 4) // PASSES < N_GROUPS:
+                copy_prepared((u + 4) // PASSES)
+            if 3 <= u < BANKS + 3:
+                empty_bank(u - 3)
+            if u >= NODE_BANKS + 2 and (u - 2) % NODE_BANKS == 0:
+                sum_senders((u - 2) // NODE_BANKS - 1)
+            if u >= NODE_BANKS + 3 and (u - 3) % NODE_BANKS == 0:
+                finish((u - 3) // NODE_BANKS - 1)

@@ -45,7 +45,7 @@ POOL_RECEIVERS = 5
 VECTOR_RECEIVERS = NODES - POOL_RECEIVERS
 POOL_COLS = GROUP * POOL_RECEIVERS
 VECTOR_COLS = GROUP * VECTOR_RECEIVERS
-VECTOR_RELU_EVERY = 5
+VECTOR_RELU_EVERY = 6
 UNITS = N_GROUPS * PASSES
 FAR_BELOW = -3.0e38
 
@@ -65,9 +65,9 @@ def tile_graphdynamics_pa_t_kernel(
         work = stack.enter_context(tc.tile_pool(name="work", bufs=2))
         deep = stack.enter_context(tc.tile_pool(name="deep", bufs=4))
         ring = stack.enter_context(tc.tile_pool(name="ring", bufs=4))
-        ps_recv = stack.enter_context(tc.psum_pool(name="ps_recv", bufs=3))
+        ps_recv = stack.enter_context(tc.psum_pool(name="ps_recv", bufs=2))
         ps_send = stack.enter_context(tc.psum_pool(name="ps_send", bufs=1))
-        ps_acc = stack.enter_context(tc.psum_pool(name="ps_acc", bufs=3))
+        ps_acc = stack.enter_context(tc.psum_pool(name="ps_acc", bufs=4))
         ps_misc = stack.enter_context(tc.psum_pool(name="ps_misc", bufs=1))
         stack.enter_context(tc.manual_schedule())
 
@@ -276,7 +276,7 @@ def tile_graphdynamics_pa_t_kernel(
             )
 
         def on_vector(unit):
-            return unit % VECTOR_RELU_EVERY == VECTOR_RELU_EVERY - 1 or unit == UNITS - 1
+            return unit % VECTOR_RELU_EVERY == VECTOR_RELU_EVERY - 1 or unit >= UNITS - PASSES
 
         def relu(grp, g):
             h = h_of[(grp, g)]
@@ -419,31 +419,35 @@ def tile_graphdynamics_pa_t_kernel(
         prepare(1)
         copy_prepared(1)
         pool_add(0, 1)
-        for u in range(UNITS + 4):
-            if u + 2 < UNITS:
-                pool_add((u + 2) // PASSES, (u + 2) % PASSES)
-            if u < UNITS:
-                vector_add(u // PASSES, u % PASSES)
-                if not on_vector(u):
-                    relu(u // PASSES, u % PASSES)
-            if 1 <= u <= UNITS and on_vector(u - 1):
-                relu((u - 1) // PASSES, (u - 1) % PASSES)
-            if u == 0:
+        for v in range(N_GROUPS + 3):
+            if v + 1 < N_GROUPS:
+                for g in range(PASSES):
+                    pool_add(v + 1, g)
+            if v < N_GROUPS:
+                for g in range(PASSES):
+                    vector_add(v, g)
+                    if not on_vector(v * PASSES + g):
+                        relu(v, g)
+            if 1 <= v <= N_GROUPS:
+                for g in range(PASSES):
+                    if on_vector((v - 1) * PASSES + g):
+                        relu(v - 1, g)
+            if v == 0:
                 mask_factors(1, N_NODE_TILES)
-                prepare(2)
-            elif u % PASSES == 1 and (u + 5) // PASSES < N_GROUPS:
-                prepare((u + 5) // PASSES)
-            if 2 <= u < UNITS + 2:
-                quantise((u - 2) // PASSES, (u - 2) % PASSES)
-                multiply((u - 2) // PASSES, (u - 2) % PASSES)
-            if u == 1:
+            if v + 2 < N_GROUPS:
+                prepare(v + 2)
+            if 1 <= v <= N_GROUPS:
+                for g in range(PASSES):
+                    quantise(v - 1, g)
+                    multiply(v - 1, g)
+            if v == 0:
                 build_surplus()
-                copy_prepared(2)
-            elif u >= 2 and u % PASSES == 0 and (u + 4) // PASSES < N_GROUPS:
-                copy_prepared((u + 4) // PASSES)
-            if 3 <= u < BANKS + 3:
-                empty_bank(u - 3)
-            if u >= NODE_BANKS + 2 and (u - 2) % NODE_BANKS == 0:
-                sum_senders((u - 2) // NODE_BANKS - 1)
-            if u >= NODE_BANKS + 3 and (u - 3) % NODE_BANKS == 0:
-                finish((u - 3) // NODE_BANKS - 1)
+            if v + 2 < N_GROUPS:
+                copy_prepared(v + 2)
+            if 2 <= v < N_GROUPS + 2:
+                for half in range(GROUP_BANKS):
+                    empty_bank((v - 2) * GROUP_BANKS + half)
+            if v >= 3 and v % 2 == 1:
+                sum_senders((v - 3) // 2)
+            if v >= 4 and v % 2 == 0:
+                finish((v - 4) // 2)

@@ -37,8 +37,6 @@ TILE_GRAPHS = NODE_TILE // NODES
 N_NODE_TILES = GRAPHS * NODES // NODE_TILE
 NODE_BANKS = NODE_TILE // BANK_ROWS
 BANKS = N_GROUPS * GROUP_BANKS
-TILE_RECEIVERS = P // NODES
-MASK_STEP = 16
 XI_SLOTS = 4
 BIAS_ROWS_END = 96
 POOL_RECEIVERS = 5
@@ -78,19 +76,18 @@ def tile_graphdynamics_pa_t_kernel(
         xj_sb = keep.tile([P, N_NODE_TILES, HIDDEN], BF16, name="xj_sb")
         w_words = keep.tile([P, PASSES, 2 * OUT_DIM], U8, name="w_words", align_bytes=64)
         w_scales = keep.tile([P, PASSES, OUT_DIM], U8, name="w_scales", align_bytes=64)
-        mask_rows = keep.tile([P, NODES], BF16, name="mask_rows")
-        mask_wide = keep.tile([P, TILE_RECEIVERS, NODES], BF16, name="mask_wide")
-        mask_col = keep.tile([P, N_NODE_TILES, MASK_STEP], BF16, name="mask_col")
+        small = keep.tile([P, P], BF16, name="small")
+        first_row = keep.tile([P, P], BF16, name="first_row")
+        first_mask = keep.tile([P, 2], BF16, name="first_mask")
         keep_col = keep.tile([P, N_NODE_TILES], F32, name="keep_col")
         drop_col = keep.tile([P, N_NODE_TILES], F32, name="drop_col")
-        bias_bf = keep.tile([P, OUT_DIM], BF16, name="bias_bf")
         relu_rows = keep.tile([P, OUT_DIM], F32, name="relu_rows")
-        bias_pair = keep.tile([P, 2], BF16, name="bias_pair")
         bias_col = keep.tile([P, 1], F32, name="bias_col")
         all_padded = keep.tile([P, 1], F32, name="all_padded")
-        same_receiver = keep.tile([P, TILE_RECEIVERS], F32, name="same_receiver")
-        sel = keep.tile([P, GRAPHS, TILE_RECEIVERS], F32, name="sel")
-        surplus = keep.tile([P, GRAPHS, NODES // TILE_RECEIVERS, TILE_RECEIVERS], F32, name="surplus")
+        same_graph = keep.tile([P, TILE_GRAPHS], F32, name="same_graph")
+        sel = keep.tile([P, N_NODE_TILES, TILE_GRAPHS], F32, name="sel")
+        surplus = keep.tile([P, GRAPHS, NODES], F32, name="surplus")
+        warm = keep.tile([P, 2], F32, name="warm")
 
         recv_of = {}
         recv_copy_of = {}
@@ -114,34 +111,33 @@ def tile_graphdynamics_pa_t_kernel(
                 out=xj_sb[:, nt, :], in_=xj_rows[nt * NODE_TILE : (nt + 1) * NODE_TILE, :]
             )
 
-        def load_mask_columns(first, end):
-            nc.scalar.dma_start(
-                out=mask_col[:, first:end, 0:1],
-                in_=node_mask.rearrange("(n b) j -> (b j) n", b=TILE_GRAPHS)[:, first:end].unsqueeze(2),
-            )
-
         nc.scalar.dma_start(
             out=xi_aug[GROUP_NODES:BIAS_ROWS_END, 0:1, :],
             in_=mb1.unsqueeze(0).unsqueeze(0).broadcast_to([BIAS_ROWS_END - GROUP_NODES, 1, HIDDEN]),
         )
-        stack.enter_context(nc.allow_non_contiguous_dma(reason="one mask or bias value to a partition"))
-        load_mask_columns(0, 1)
-        nc.vector.memset(mask_rows[:], 0.0)
+        stack.enter_context(nc.allow_non_contiguous_dma(reason="one mask value to a partition"))
+        nc.scalar.dma_start(
+            out=first_mask[:, 0:1],
+            in_=node_mask[0:TILE_GRAPHS, :].rearrange("b j -> (b j)").unsqueeze(1),
+        )
+        nc.vector.memset(warm[:], 0.0)
+        nc.scalar.activation(out=warm[:, 1:2], in_=warm[:, 0:1], func=ACT.Relu)
+        nc.vector.memset(small[:], 0.0)
         nc.vector.memset(xi_aug[BIAS_ROWS_END:P, 0:1, :].bitcast(I32), 0)
         nc.vector.memset(w_scales[:].bitcast(I32), 0)
         nc.vector.memset(xi_aug[GROUP_NODES:P, 1:XI_SLOTS, :].bitcast(I32), 0)
 
-        nc.scalar.dma_start(out=bias_bf[:], in_=mb2.partition_broadcast(P))
-        nc.scalar.dma_start(out=mask_rows[0:GRAPHS, :], in_=node_mask)
         nc.scalar.dma_start(
             out=xi_aug[GROUP_NODES : GROUP_NODES + 1, 1:XI_SLOTS, :],
             in_=mb1.unsqueeze(0).unsqueeze(0).broadcast_to([1, XI_SLOTS - 1, HIDDEN]),
         )
-        load_mask_columns(1, N_NODE_TILES)
-        nc.scalar.dma_start(out=bias_pair[:, 0:1], in_=mb2.rearrange("(d o) -> d o", o=1))
 
         load_receivers(0)
         load_senders(0)
+        nc.sync.dma_start(
+            out=small[1 : 1 + N_NODE_TILES, :], in_=node_mask.rearrange("(n b) j -> n (b j)", b=TILE_GRAPHS)
+        )
+        nc.sync.dma_start(out=small[0:1, :], in_=mb2.unsqueeze(0))
         load_receivers(1)
         for g in range(PASSES):
             nc.sync.dma_start(out=w_words[:, g, :].bitcast(I32), in_=mw2_words[g].bitcast(I32))
@@ -170,14 +166,34 @@ def tile_graphdynamics_pa_t_kernel(
         )
         nc.vector.memset(pick[GROUP_NODES : GROUP_NODES + 1, :], 1.0)
 
-        def mask_factors(first, end):
-            nc.vector.tensor_copy(out=keep_col[:, first:end], in_=mask_col[:, first:end, 0])
+        def mask_factors(first, end, values):
+            nc.vector.tensor_copy(out=keep_col[:, first:end], in_=values)
             nc.vector.tensor_scalar(
                 out=drop_col[:, first:end],
-                in0=mask_col[:, first:end, 0],
+                in0=values,
                 scalar1=-1.0,
                 scalar2=-FAR_BELOW,
                 op0=ALU.add,
+                op1=ALU.mult,
+            )
+
+        small_of = {}
+
+        def turn_small():
+            small_turned = ps_misc.tile([P, P], BF16, name="small_turned", tag="misc")
+            small_of[0] = small_turned
+            nc.tensor.transpose(out=small_turned[:], in_=small[:], identity=ident_bf[:])
+
+        def read_small():
+            small_turned = small_of[0]
+            mask_factors(1, N_NODE_TILES, small_turned[:, 2 : 1 + N_NODE_TILES])
+            nc.vector.tensor_copy(out=bias_col[:], in_=small_turned[:, 0:1])
+            nc.vector.tensor_scalar(
+                out=all_padded[:],
+                in0=small_turned[:, 0:1],
+                scalar1=0.0,
+                scalar2=-1.0 * NODES,
+                op0=ALU.max,
                 op1=ALU.mult,
             )
 
@@ -276,7 +292,7 @@ def tile_graphdynamics_pa_t_kernel(
             )
 
         def on_vector(unit):
-            return unit % VECTOR_RELU_EVERY == VECTOR_RELU_EVERY - 1 or unit >= UNITS - PASSES
+            return unit % VECTOR_RELU_EVERY == VECTOR_RELU_EVERY - 1 or unit == UNITS - 1
 
         def relu(grp, g):
             h = h_of[(grp, g)]
@@ -326,9 +342,7 @@ def tile_graphdynamics_pa_t_kernel(
             total_of[nt] = total
             nc.tensor.matmul(
                 out=total[:],
-                lhsT=surplus[:, nt * TILE_GRAPHS : (nt + 1) * TILE_GRAPHS, :, :].rearrange(
-                    "p b s i -> p (b s i)"
-                ),
+                lhsT=surplus[:, nt * TILE_GRAPHS : (nt + 1) * TILE_GRAPHS, :].rearrange("p b i -> p (b i)"),
                 rhs=ident_f32[:],
                 start=True,
                 stop=False,
@@ -349,53 +363,41 @@ def tile_graphdynamics_pa_t_kernel(
             nc.scalar.copy(out=result[:], in_=total_of[nt][:])
             nc.sync.dma_start(out=out_rows[nt * NODE_TILE : (nt + 1) * NODE_TILE, :], in_=result[:])
 
-        def build_selection():
-            nc.vector.tensor_scalar_max(out=relu_rows[:], in0=bias_bf[:], scalar1=0.0)
-            nc.vector.tensor_copy(
-                out=mask_wide[:],
-                in_=mask_rows[:].unsqueeze(1).broadcast_to([P, TILE_RECEIVERS, NODES]),
-            )
-            mask_turned = ps_misc.tile([P, P], BF16, name="mask_turned", tag="misc")
-            nc.tensor.transpose(
-                out=mask_turned[:], in_=mask_wide[:].rearrange("p r j -> p (r j)"), identity=ident_bf[:]
-            )
+        spread_of = {}
+
+        def begin_surplus():
+            nc.vector.memset(first_row[:], 0.0)
+            nc.vector.memset(first_row[0:1, :], 1.0)
+            spread = ps_misc.tile([P, OUT_DIM], F32, name="spread", tag="misc")
+            spread_of[0] = spread
+            nc.tensor.matmul(out=spread[:], lhsT=first_row[:], rhs=small[:], start=True, stop=True)
             nc.vector.tensor_reduce(
-                out=same_receiver[:],
-                in_=ident_f32[:].rearrange("p (i j) -> p i j", j=NODES),
+                out=same_graph[:],
+                in_=ident_f32[:].rearrange("p (b j) -> p b j", j=NODES),
                 axis=AXIS.X,
                 op=ALU.add,
             )
+            shape = [P, N_NODE_TILES, TILE_GRAPHS]
             nc.vector.tensor_tensor(
                 out=sel[:],
-                in0=mask_turned[:, 0:GRAPHS].unsqueeze(2).broadcast_to([P, GRAPHS, TILE_RECEIVERS]),
-                in1=same_receiver[:].unsqueeze(1).broadcast_to([P, GRAPHS, TILE_RECEIVERS]),
+                in0=keep_col[:].unsqueeze(2).broadcast_to(shape),
+                in1=same_graph[:].unsqueeze(1).broadcast_to(shape),
                 op=ALU.mult,
             )
 
-        def build_surplus():
-            nc.vector.tensor_copy(out=bias_col[:], in_=bias_pair[:, 0:1])
-            nc.vector.tensor_scalar(
-                out=all_padded[:],
-                in0=bias_pair[:, 0:1],
-                scalar1=0.0,
-                scalar2=-1.0 * NODES,
-                op0=ALU.max,
-                op1=ALU.mult,
-            )
-            share = ps_misc.tile([P, GRAPHS * TILE_RECEIVERS], F32, name="share", tag="misc")
+        def end_surplus():
+            nc.vector.tensor_scalar_max(out=relu_rows[:], in0=spread_of[0][:], scalar1=0.0)
+            share = ps_misc.tile([P, GRAPHS], F32, name="share", tag="misc")
             nc.tensor.matmul(
                 out=share[:],
                 lhsT=relu_rows[:],
-                rhs=sel[:].rearrange("p b i -> p (b i)"),
+                rhs=sel[:].rearrange("p n b -> p (n b)"),
                 start=True,
                 stop=True,
             )
             nc.scalar.activation(
                 out=surplus[:],
-                in_=share[:]
-                .rearrange("p (b i) -> p b i", i=TILE_RECEIVERS)
-                .unsqueeze(2)
-                .broadcast_to([P, GRAPHS, NODES // TILE_RECEIVERS, TILE_RECEIVERS]),
+                in_=share[:].unsqueeze(2).broadcast_to([P, GRAPHS, NODES]),
                 func=ACT.Identity,
                 bias=all_padded[:, 0:1],
             )
@@ -411,14 +413,16 @@ def tile_graphdynamics_pa_t_kernel(
                 copy_senders(grp // 2)
             copy_receivers(grp)
 
-        mask_factors(0, 1)
+        mask_factors(0, 1, first_mask[:, 0:1])
         prepare(0)
         copy_prepared(0)
         pool_add(0, 0)
-        build_selection()
+        turn_small()
         prepare(1)
         copy_prepared(1)
         pool_add(0, 1)
+        read_small()
+        begin_surplus()
         for v in range(N_GROUPS + 3):
             if v + 1 < N_GROUPS:
                 for g in range(PASSES):
@@ -433,15 +437,13 @@ def tile_graphdynamics_pa_t_kernel(
                     if on_vector((v - 1) * PASSES + g):
                         relu(v - 1, g)
             if v == 0:
-                mask_factors(1, N_NODE_TILES)
+                end_surplus()
             if v + 2 < N_GROUPS:
                 prepare(v + 2)
             if 1 <= v <= N_GROUPS:
                 for g in range(PASSES):
                     quantise(v - 1, g)
                     multiply(v - 1, g)
-            if v == 0:
-                build_surplus()
             if v + 2 < N_GROUPS:
                 copy_prepared(v + 2)
             if 2 <= v < N_GROUPS + 2:

@@ -44,6 +44,10 @@ VECTOR_RECEIVERS = NODES - POOL_RECEIVERS
 POOL_COLS = GROUP * POOL_RECEIVERS
 VECTOR_COLS = GROUP * VECTOR_RECEIVERS
 VECTOR_RELU_EVERY = 6
+TENSOR_GRAPHS = 2
+TENSOR_NODES = TENSOR_GRAPHS * NODES
+TENSOR_PAIRS = TENSOR_GRAPHS * NODES * NODES
+CHUNK_PAIRS = P
 UNITS = N_GROUPS * PASSES
 FAR_BELOW = -3.0e38
 
@@ -79,6 +83,10 @@ def tile_graphdynamics_pa_t_kernel(
         small = keep.tile([P, P], BF16, name="small")
         first_row = keep.tile([P, P], BF16, name="first_row")
         first_mask = keep.tile([P, 2], BF16, name="first_mask")
+        moved_mask = keep.tile([P, 2], BF16, name="moved_mask")
+        moved_keep = keep.tile([P, 1], F32, name="moved_keep")
+        moved_drop = keep.tile([P, 1], F32, name="moved_drop")
+        pair_pick = keep.tile([P, TENSOR_PAIRS], BF16, name="pair_pick")
         keep_col = keep.tile([P, N_NODE_TILES], F32, name="keep_col")
         drop_col = keep.tile([P, N_NODE_TILES], F32, name="drop_col")
         relu_rows = keep.tile([P, OUT_DIM], F32, name="relu_rows")
@@ -120,10 +128,13 @@ def tile_graphdynamics_pa_t_kernel(
             out=first_mask[:, 0:1],
             in_=node_mask[0:TILE_GRAPHS, :].rearrange("b j -> (b j)").unsqueeze(1),
         )
+        nc.scalar.dma_start(
+            out=moved_mask[BIAS_ROWS_END:P, 0:1],
+            in_=node_mask[0:TENSOR_GRAPHS, :].rearrange("b j -> (b j)").unsqueeze(1),
+        )
         nc.vector.memset(warm[:], 0.0)
         nc.scalar.activation(out=warm[:, 1:2], in_=warm[:, 0:1], func=ACT.Relu)
         nc.vector.memset(small[:], 0.0)
-        nc.vector.memset(xi_aug[BIAS_ROWS_END:P, 0:1, :].bitcast(I32), 0)
         nc.vector.memset(w_scales[:].bitcast(I32), 0)
         nc.vector.memset(xi_aug[GROUP_NODES:P, 1:XI_SLOTS, :].bitcast(I32), 0)
 
@@ -133,6 +144,7 @@ def tile_graphdynamics_pa_t_kernel(
         )
 
         load_receivers(0)
+        nc.sync.dma_start(out=xi_aug[BIAS_ROWS_END:P, 0, :], in_=xj_rows[0:TENSOR_NODES, :])
         load_senders(0)
         nc.sync.dma_start(
             out=small[1 : 1 + N_NODE_TILES, :], in_=node_mask.rearrange("(n b) j -> n (b j)", b=TILE_GRAPHS)
@@ -219,7 +231,7 @@ def tile_graphdynamics_pa_t_kernel(
                     start=True,
                     stop=True,
                 )
-            if grp + XI_SLOTS < N_GROUPS:
+            if 0 < grp < N_GROUPS - XI_SLOTS:
                 load_receivers(grp + XI_SLOTS)
 
         def copy_receivers(grp):
@@ -266,40 +278,103 @@ def tile_graphdynamics_pa_t_kernel(
                 "p (b i j t) -> p b i j t", b=GROUP, i=NODES, j=NODES
             )
 
+        def first_graph(grp):
+            return TENSOR_GRAPHS if grp == 0 else 0
+
         def pool_add(grp, g):
             h_of[(grp, g)] = ring.tile([P, GROUP_PAIRS * PACK], BF16, name="h", align_bytes=64)
-            shape = [P, GROUP, POOL_RECEIVERS, NODES, PACK]
+            b0 = first_graph(grp)
+            shape = [P, GROUP - b0, POOL_RECEIVERS, NODES, PACK]
             nc.gpsimd.tensor_tensor(
-                out=pairs_of(grp, g)[:, :, VECTOR_RECEIVERS:NODES],
+                out=pairs_of(grp, g)[:, b0:GROUP, VECTOR_RECEIVERS:NODES],
                 in0=recv_copy_of[grp][:, g, :, :]
-                .rearrange("p (b i) t -> p b i t", b=GROUP)
+                .rearrange("p (b i) t -> p b i t", b=GROUP)[:, b0:GROUP]
                 .unsqueeze(3)
                 .broadcast_to(shape),
-                in1=senders_of(grp, g).unsqueeze(2).broadcast_to(shape),
+                in1=senders_of(grp, g)[:, b0:GROUP].unsqueeze(2).broadcast_to(shape),
                 op=ALU.add,
             )
 
         def vector_add(grp, g):
-            shape = [P, GROUP, VECTOR_RECEIVERS, NODES, PACK]
+            b0 = first_graph(grp)
+            shape = [P, GROUP - b0, VECTOR_RECEIVERS, NODES, PACK]
             nc.vector.tensor_tensor(
-                out=pairs_of(grp, g)[:, :, 0:VECTOR_RECEIVERS],
+                out=pairs_of(grp, g)[:, b0:GROUP, 0:VECTOR_RECEIVERS],
                 in0=recv_of[grp][:, PACK * g : PACK * (g + 1), 0:VECTOR_COLS]
-                .rearrange("p t (b i) -> p b i t", b=GROUP)
+                .rearrange("p t (b i) -> p b i t", b=GROUP)[:, b0:GROUP]
                 .unsqueeze(3)
                 .broadcast_to(shape),
-                in1=senders_of(grp, g).unsqueeze(2).broadcast_to(shape),
+                in1=senders_of(grp, g)[:, b0:GROUP].unsqueeze(2).broadcast_to(shape),
                 op=ALU.add,
             )
+
+        def build_pair_pick():
+            shape = [P, TENSOR_GRAPHS, NODES, NODES]
+            nc.vector.tensor_tensor(
+                out=pair_pick[:].rearrange("p (b i j) -> p b i j", b=TENSOR_GRAPHS, i=NODES),
+                in0=ident_bf[:, 0:TENSOR_NODES]
+                .rearrange("p (b i) -> p b i", b=TENSOR_GRAPHS)
+                .unsqueeze(3)
+                .broadcast_to(shape),
+                in1=ident_bf[:, BIAS_ROWS_END:P]
+                .rearrange("p (b j) -> p b j", b=TENSOR_GRAPHS)
+                .unsqueeze(2)
+                .broadcast_to(shape),
+                op=ALU.add,
+            )
+            nc.vector.memset(pair_pick[GROUP_NODES : GROUP_NODES + 1, :], 1.0)
+
+        def mask_moved_senders():
+            rows = slice(BIAS_ROWS_END, P)
+            nc.vector.tensor_copy(out=moved_keep[rows, :], in_=moved_mask[rows, 0:1])
+            nc.vector.tensor_scalar(
+                out=moved_drop[rows, :],
+                in0=moved_mask[rows, 0:1],
+                scalar1=-1.0,
+                scalar2=-FAR_BELOW,
+                op0=ALU.add,
+                op1=ALU.mult,
+            )
+            nc.vector.tensor_scalar(
+                out=xi_aug[rows, 0, :],
+                in0=xi_aug[rows, 0, :],
+                scalar1=moved_keep[rows, 0:1],
+                scalar2=moved_drop[rows, 0:1],
+                op0=ALU.mult,
+                op1=ALU.add,
+            )
+
+        def tensor_add(g):
+            sums = {}
+            for c in range(TENSOR_PAIRS // CHUNK_PAIRS):
+                sums[c] = ps_acc.tile([P, PACK, CHUNK_PAIRS], F32, name="acc")
+            for c in range(TENSOR_PAIRS // CHUNK_PAIRS):
+                for t in range(PACK):
+                    nc.tensor.matmul(
+                        out=sums[c][:, t, :],
+                        lhsT=xi_aug[:, 0, K_PASS * g + t : K_PASS * (g + 1) : PACK],
+                        rhs=pair_pick[:, c * CHUNK_PAIRS : (c + 1) * CHUNK_PAIRS],
+                        start=True,
+                        stop=True,
+                    )
+            for c in range(TENSOR_PAIRS // CHUNK_PAIRS):
+                nc.scalar.activation(
+                    out=h_of[(0, g)][:, c * CHUNK_PAIRS * PACK : (c + 1) * CHUNK_PAIRS * PACK].rearrange(
+                        "p (n t) -> p n t", t=PACK
+                    ),
+                    in_=sums[c][:].rearrange("p t n -> p n t"),
+                    func=ACT.Relu,
+                )
 
         def on_vector(unit):
             return unit % VECTOR_RELU_EVERY == VECTOR_RELU_EVERY - 1 or unit == UNITS - 1
 
         def relu(grp, g):
-            h = h_of[(grp, g)]
+            h = h_of[(grp, g)][:, first_graph(grp) * NODES * NODES * PACK :]
             if on_vector(grp * PASSES + g):
-                nc.vector.tensor_scalar_max(out=h[:], in0=h[:], scalar1=0.0)
+                nc.vector.tensor_scalar_max(out=h, in0=h, scalar1=0.0)
             else:
-                nc.scalar.activation(out=h[:], in_=h[:], func=ACT.Relu)
+                nc.scalar.activation(out=h, in_=h, func=ACT.Relu)
 
         def quantise(grp, g):
             codes = deep.tile([P, GROUP_PAIRS], U32, name="codes", align_bytes=64)
@@ -418,6 +493,9 @@ def tile_graphdynamics_pa_t_kernel(
         copy_prepared(0)
         pool_add(0, 0)
         turn_small()
+        build_pair_pick()
+        mask_moved_senders()
+        tensor_add(0)
         prepare(1)
         copy_prepared(1)
         pool_add(0, 1)
@@ -432,6 +510,9 @@ def tile_graphdynamics_pa_t_kernel(
                     vector_add(v, g)
                     if not on_vector(v * PASSES + g):
                         relu(v, g)
+                    if v == 0 and g == 0:
+                        tensor_add(1)
+                        load_receivers(XI_SLOTS)
             if 1 <= v <= N_GROUPS:
                 for g in range(PASSES):
                     if on_vector((v - 1) * PASSES + g):

@@ -37,7 +37,7 @@ TILE_GRAPHS = NODE_TILE // NODES
 N_NODE_TILES = GRAPHS * NODES // NODE_TILE
 NODE_BANKS = NODE_TILE // BANK_ROWS
 BANKS = N_GROUPS * GROUP_BANKS
-XI_SLOTS = 4
+XI_SLOTS = 2
 BIAS_ROWS_END = 96
 POOL_RECEIVERS = 5
 VECTOR_RECEIVERS = NODES - POOL_RECEIVERS
@@ -160,8 +160,6 @@ def tile_graphdynamics_pa_t_kernel(
                 .rearrange("g q n -> q g n")
                 .bitcast(I32),
             )
-        load_receivers(2)
-        load_receivers(3)
         for nt in range(1, N_NODE_TILES):
             load_senders(nt)
 
@@ -440,18 +438,20 @@ def tile_graphdynamics_pa_t_kernel(
 
         spread_of = {}
 
-        def begin_surplus():
+        def surplus_constants():
             nc.vector.memset(first_row[:], 0.0)
             nc.vector.memset(first_row[0:1, :], 1.0)
-            spread = ps_misc.tile([P, OUT_DIM], F32, name="spread", tag="misc")
-            spread_of[0] = spread
-            nc.tensor.matmul(out=spread[:], lhsT=first_row[:], rhs=small[:], start=True, stop=True)
             nc.vector.tensor_reduce(
                 out=same_graph[:],
                 in_=ident_f32[:].rearrange("p (b j) -> p b j", j=NODES),
                 axis=AXIS.X,
                 op=ALU.add,
             )
+
+        def begin_surplus():
+            spread = ps_misc.tile([P, OUT_DIM], F32, name="spread", tag="misc")
+            spread_of[0] = spread
+            nc.tensor.matmul(out=spread[:], lhsT=first_row[:], rhs=small[:], start=True, stop=True)
             shape = [P, N_NODE_TILES, TILE_GRAPHS]
             nc.vector.tensor_tensor(
                 out=sel[:],
@@ -488,12 +488,13 @@ def tile_graphdynamics_pa_t_kernel(
                 copy_senders(grp // 2)
             copy_receivers(grp)
 
+        build_pair_pick()
+        surplus_constants()
         mask_factors(0, 1, first_mask[:, 0:1])
         prepare(0)
         copy_prepared(0)
         pool_add(0, 0)
         turn_small()
-        build_pair_pick()
         mask_moved_senders()
         tensor_add(0)
         prepare(1)

from contextlib import ExitStack

import concourse.mybir as mybir
from concourse.masks import make_identity

F32 = mybir.dt.float32
BF16 = mybir.dt.bfloat16
I32 = mybir.dt.int32
U32 = mybir.dt.uint32
U8 = mybir.dt.uint8
FP8X4 = mybir.dt.float8_e4m3fn_x4
FP4X4 = mybir.dt.float4_e2m1fn_x4
ALU = mybir.AluOpType
ACT = mybir.ActivationFunctionType
AXIS = mybir.AxisListType

GRAPHS = 64
NODES = 16
HIDDEN = 1024
OUT_DIM = 128

P = 128
PACK = 4
K_PASS = P * PACK
PASSES = HIDDEN // K_PASS
PLANES = PASSES * PACK

GROUP = 4
GROUP_NODES = GROUP * NODES
GROUP_PAIRS = GROUP * NODES * NODES
N_GROUPS = GRAPHS // GROUP
BANK_PAIRS = 512
GROUP_BANKS = GROUP_PAIRS // BANK_PAIRS
BANK_ROWS = BANK_PAIRS // NODES
NODE_TILE = P
TILE_GRAPHS = NODE_TILE // NODES
N_NODE_TILES = GRAPHS * NODES // NODE_TILE
NODE_BANKS = NODE_TILE // BANK_ROWS
BANKS = N_GROUPS * GROUP_BANKS
XI_SLOTS = 2
BIAS_ROWS_END = 96
POOL_RECEIVERS = 5
VECTOR_RECEIVERS = NODES - POOL_RECEIVERS
POOL_COLS = GROUP * POOL_RECEIVERS
VECTOR_COLS = GROUP * VECTOR_RECEIVERS
VECTOR_RELU_EVERY = 6
TENSOR_GRAPHS = 2
TENSOR_NODES = TENSOR_GRAPHS * NODES
TENSOR_PAIRS = TENSOR_GRAPHS * NODES * NODES
CHUNK_PAIRS = P
UNITS = N_GROUPS * PASSES
FAR_BELOW = -3.0e38

FLOPS = 2 * GRAPHS * NODES * NODES * HIDDEN * OUT_DIM


def tile_graphdynamics_pa_t_kernel(
    tc, xi_p, xj_p, node_mask, mb1, mw2_words, mw2_scales, mb2, out
):
    nc = tc.nc
    xi_rows = xi_p.rearrange("b n h -> (b n) h")
    xj_rows = xj_p.rearrange("b n h -> (b n) h")
    out_rows = out.rearrange("b n d -> (b n) d")

    with ExitStack() as stack:
        keep = stack.enter_context(tc.tile_pool(name="keep", bufs=1))
        work = stack.enter_context(tc.tile_pool(name="work", bufs=2))
        deep = stack.enter_context(tc.tile_pool(name="deep", bufs=4))
        ring = stack.enter_context(tc.tile_pool(name="ring", bufs=4))
        ps_recv = stack.enter_context(tc.psum_pool(name="ps_recv", bufs=2))
        ps_send = stack.enter_context(tc.psum_pool(name="ps_send", bufs=1))
        ps_acc = stack.enter_context(tc.psum_pool(name="ps_acc", bufs=4))
        ps_misc = stack.enter_context(tc.psum_pool(name="ps_misc", bufs=1))
        stack.enter_context(tc.manual_schedule())

        ident_bf = keep.tile([P, P], BF16, name="ident_bf")
        ident_f32 = keep.tile([P, P], F32, name="ident_f32")
        pick = keep.tile([P, GROUP_NODES], BF16, name="pick")
        xi_aug = keep.tile([P, XI_SLOTS, HIDDEN], BF16, name="xi_aug")
        xj_sb = keep.tile([P, N_NODE_TILES, HIDDEN], BF16, name="xj_sb")
        w_words = keep.tile([P, PASSES, 2 * OUT_DIM], U8, name="w_words", align_bytes=64)
        w_scales = keep.tile([P, PASSES, OUT_DIM], U8, name="w_scales", align_bytes=64)
        small = keep.tile([P, P], BF16, name="small")
        first_row = keep.tile([P, P], BF16, name="first_row")
        first_mask = keep.tile([P, 2], BF16, name="first_mask")
        moved_mask = keep.tile([P, 2], BF16, name="moved_mask")
        moved_keep = keep.tile([P, 1], F32, name="moved_keep")
        moved_drop = keep.tile([P, 1], F32, name="moved_drop")
        pair_pick = keep.tile([P, TENSOR_PAIRS], BF16, name="pair_pick")
        keep_col = keep.tile([P, N_NODE_TILES], F32, name="keep_col")
        drop_col = keep.tile([P, N_NODE_TILES], F32, name="drop_col")
        relu_rows = keep.tile([P, OUT_DIM], F32, name="relu_rows")
        bias_col = keep.tile([P, 1], F32, name="bias_col")
        all_padded = keep.tile([P, 1], F32, name="all_padded")
        same_graph = keep.tile([P, TILE_GRAPHS], F32, name="same_graph")
        sel = keep.tile([P, N_NODE_TILES, TILE_GRAPHS], F32, name="sel")
        surplus = keep.tile([P, GRAPHS, NODES], F32, name="surplus")
        warm = keep.tile([P, 2], F32, name="warm")

        recv_of = {}
        recv_copy_of = {}
        turned_of = {}
        send_of = {}
        h_of = {}
        codes_of = {}
        scales_of = {}
        acc_of = {}
        msgs_of = {}
        total_of = {}

        def load_receivers(grp):
            nc.sync.dma_start(
                out=xi_aug[0:GROUP_NODES, grp % XI_SLOTS, :],
                in_=xi_rows[grp * GROUP_NODES : (grp + 1) * GROUP_NODES, :],
            )

        def load_senders(nt):
            nc.sync.dma_start(
                out=xj_sb[:, nt, :], in_=xj_rows[nt * NODE_TILE : (nt + 1) * NODE_TILE, :]
            )

        nc.scalar.dma_start(
            out=xi_aug[GROUP_NODES:BIAS_ROWS_END, 0:1, :],
            in_=mb1.unsqueeze(0).unsqueeze(0).broadcast_to([BIAS_ROWS_END - GROUP_NODES, 1, HIDDEN]),
        )
        stack.enter_context(nc.allow_non_contiguous_dma(reason="one mask value to a partition"))
        nc.scalar.dma_start(
            out=first_mask[:, 0:1],
            in_=node_mask[0:TILE_GRAPHS, :].rearrange("b j -> (b j)").unsqueeze(1),
        )
        nc.scalar.dma_start(
            out=moved_mask[BIAS_ROWS_END:P, 0:1],
            in_=node_mask[0:TENSOR_GRAPHS, :].rearrange("b j -> (b j)").unsqueeze(1),
        )
        nc.vector.memset(warm[:], 0.0)
        nc.scalar.activation(out=warm[:, 1:2], in_=warm[:, 0:1], func=ACT.Relu)
        nc.vector.memset(small[:], 0.0)
        nc.vector.memset(w_scales[:].bitcast(I32), 0)
        nc.vector.memset(xi_aug[GROUP_NODES:P, 1:XI_SLOTS, :].bitcast(I32), 0)

        nc.scalar.dma_start(
            out=xi_aug[GROUP_NODES : GROUP_NODES + 1, 1:XI_SLOTS, :],
            in_=mb1.unsqueeze(0).unsqueeze(0).broadcast_to([1, XI_SLOTS - 1, HIDDEN]),
        )

        load_receivers(0)
        nc.sync.dma_start(out=xi_aug[BIAS_ROWS_END:P, 0, :], in_=xj_rows[0:TENSOR_NODES, :])
        load_senders(0)
        nc.sync.dma_start(
            out=small[1 : 1 + N_NODE_TILES, :], in_=node_mask.rearrange("(n b) j -> n (b j)", b=TILE_GRAPHS)
        )
        nc.sync.dma_start(out=small[0:1, :], in_=mb2.unsqueeze(0))
        load_receivers(1)
        for g in range(PASSES):
            nc.sync.dma_start(out=w_words[:, g, :].bitcast(I32), in_=mw2_words[g].bitcast(I32))
        for quad in range(4):
            nc.sync.dma_start(
                out=w_scales[32 * quad : 32 * quad + 4, :, :].bitcast(I32),
                in_=mw2_scales[:, 4 * quad : 4 * quad + 4, :]
                .rearrange("g q n -> q g n")
                .bitcast(I32),
            )
        for nt in range(1, N_NODE_TILES):
            load_senders(nt)

        make_identity(nc, ident_bf[:])
        make_identity(nc, ident_f32[:])
        by_graph = ident_bf[:, 0:GROUP_NODES].rearrange("p (b i) -> p b i", b=GROUP)
        nc.vector.tensor_copy(
            out=pick[:, 0:VECTOR_COLS].rearrange("p (b i) -> p b i", b=GROUP),
            in_=by_graph[:, :, 0:VECTOR_RECEIVERS],
        )
        nc.vector.tensor_copy(
            out=pick[:, VECTOR_COLS:GROUP_NODES].rearrange("p (b i) -> p b i", b=GROUP),
            in_=by_graph[:, :, VECTOR_RECEIVERS:NODES],
        )
        nc.vector.memset(pick[GROUP_NODES : GROUP_NODES + 1, :], 1.0)

        def mask_factors(first, end, values):
            nc.vector.tensor_copy(out=keep_col[:, first:end], in_=values)
            nc.vector.tensor_scalar(
                out=drop_col[:, first:end],
                in0=values,
                scalar1=-1.0,
                scalar2=-FAR_BELOW,
                op0=ALU.add,
                op1=ALU.mult,
            )

        small_of = {}

        def turn_small():
            small_turned = ps_misc.tile([P, P], BF16, name="small_turned", tag="misc")
            small_of[0] = small_turned
            nc.tensor.transpose(out=small_turned[:], in_=small[:], identity=ident_bf[:])

        def read_small():
            small_turned = small_of[0]
            mask_factors(1, N_NODE_TILES, small_turned[:, 2 : 1 + N_NODE_TILES])
            nc.vector.tensor_copy(out=bias_col[:], in_=small_turned[:, 0:1])
            nc.vector.tensor_scalar(
                out=all_padded[:],
                in0=small_turned[:, 0:1],
                scalar1=0.0,
                scalar2=-1.0 * NODES,
                op0=ALU.max,
                op1=ALU.mult,
            )

        def mask_senders(nt):
            nc.vector.tensor_scalar(
                out=xj_sb[:, nt, :],
                in0=xj_sb[:, nt, :],
                scalar1=keep_col[:, nt : nt + 1],
                scalar2=drop_col[:, nt : nt + 1],
                op0=ALU.mult,
                op1=ALU.add,
            )

        def prepare_receivers(grp):
            recv = ps_recv.tile([P, PLANES, GROUP_NODES], F32, name="recv")
            recv_of[grp] = recv
            for plane in range(PLANES):
                g, t = divmod(plane, PACK)
                nc.tensor.matmul(
                    out=recv[:, plane, :],
                    lhsT=xi_aug[:, grp % XI_SLOTS, K_PASS * g + t : K_PASS * (g + 1) : PACK],
                    rhs=pick[:],
                    start=True,
                    stop=True,
                )
            if 0 < grp < N_GROUPS - XI_SLOTS:
                load_receivers(grp + XI_SLOTS)

        def copy_receivers(grp):
            recv_copy = deep.tile([P, PASSES, POOL_COLS, PACK], F32, name="recv_copy")
            recv_copy_of[grp] = recv_copy
            nc.scalar.copy(
                out=recv_copy[:],
                in_=recv_of[grp][:, :, VECTOR_COLS:GROUP_NODES].rearrange(
                    "p (g t) n -> p g n t", t=PACK
                ),
            )

        def turn_senders(nt):
            words = xj_sb[:, nt, :].bitcast(F32)
            turned = ps_send.tile([P, PASSES * 2, NODE_TILE], F32, name="turned")
            turned_of[nt] = turned
            for half_plane in range(PASSES * 2):
                g, u = divmod(half_plane, 2)
                nc.tensor.transpose(
                    out=turned[:, half_plane, :],
                    in_=words[:, (K_PASS // 2) * g + u : (K_PASS // 2) * (g + 1) : 2],
                    identity=ident_f32[:],
                )

        def copy_senders(nt):
            send = work.tile([P, PASSES, NODE_TILE, PACK], BF16, name="send")
            send_of[nt] = send
            nc.scalar.copy(
                out=send[:]
                .rearrange("p g n t -> p (g n t)")
                .bitcast(F32)
                .rearrange("p (g n u) -> p g n u", g=PASSES, u=2),
                in_=turned_of[nt][:].rearrange("p (g u) n -> p g n u", u=2),
            )

        def senders_of(grp, g):
            first = (grp % 2) * GROUP_NODES
            return send_of[grp // 2][:, g, first : first + GROUP_NODES, :].rearrange(
                "p (b j) t -> p b j t", b=GROUP
            )

        def pairs_of(grp, g):
            return h_of[(grp, g)][:].rearrange(
                "p (b i j t) -> p b i j t", b=GROUP, i=NODES, j=NODES
            )

        def first_graph(grp):
            return TENSOR_GRAPHS if grp == 0 else 0

        def pool_add(grp, g):
            h_of[(grp, g)] = ring.tile([P, GROUP_PAIRS * PACK], BF16, name="h", align_bytes=64)
            b0 = first_graph(grp)
            shape = [P, GROUP - b0, POOL_RECEIVERS, NODES, PACK]
            nc.gpsimd.tensor_tensor(
                out=pairs_of(grp, g)[:, b0:GROUP, VECTOR_RECEIVERS:NODES],
                in0=recv_copy_of[grp][:, g, :, :]
                .rearrange("p (b i) t -> p b i t", b=GROUP)[:, b0:GROUP]
                .unsqueeze(3)
                .broadcast_to(shape),
                in1=senders_of(grp, g)[:, b0:GROUP].unsqueeze(2).broadcast_to(shape),
                op=ALU.add,
            )

        def vector_add(grp, g):
            b0 = first_graph(grp)
            shape = [P, GROUP - b0, VECTOR_RECEIVERS, NODES, PACK]
            nc.vector.tensor_tensor(
                out=pairs_of(grp, g)[:, b0:GROUP, 0:VECTOR_RECEIVERS],
                in0=recv_of[grp][:, PACK * g : PACK * (g + 1), 0:VECTOR_COLS]
                .rearrange("p t (b i) -> p b i t", b=GROUP)[:, b0:GROUP]
                .unsqueeze(3)
                .broadcast_to(shape),
                in1=senders_of(grp, g)[:, b0:GROUP].unsqueeze(2).broadcast_to(shape),
                op=ALU.add,
            )

        def build_pair_pick():
            shape = [P, TENSOR_GRAPHS, NODES, NODES]
            nc.vector.tensor_tensor(
                out=pair_pick[:].rearrange("p (b i j) -> p b i j", b=TENSOR_GRAPHS, i=NODES),
                in0=ident_bf[:, 0:TENSOR_NODES]
                .rearrange("p (b i) -> p b i", b=TENSOR_GRAPHS)
                .unsqueeze(3)
                .broadcast_to(shape),
                in1=ident_bf[:, BIAS_ROWS_END:P]
                .rearrange("p (b j) -> p b j", b=TENSOR_GRAPHS)
                .unsqueeze(2)
                .broadcast_to(shape),
                op=ALU.add,
            )
            nc.vector.memset(pair_pick[GROUP_NODES : GROUP_NODES + 1, :], 1.0)

        def mask_moved_senders():
            rows = slice(BIAS_ROWS_END, P)
            nc.vector.tensor_copy(out=moved_keep[rows, :], in_=moved_mask[rows, 0:1])
            nc.vector.tensor_scalar(
                out=moved_drop[rows, :],
                in0=moved_mask[rows, 0:1],
                scalar1=-1.0,
                scalar2=-FAR_BELOW,
                op0=ALU.add,
                op1=ALU.mult,
            )
            nc.vector.tensor_scalar(
                out=xi_aug[rows, 0, :],
                in0=xi_aug[rows, 0, :],
                scalar1=moved_keep[rows, 0:1],
                scalar2=moved_drop[rows, 0:1],
                op0=ALU.mult,
                op1=ALU.add,
            )

        def tensor_add(g):
            sums = {}
            for c in range(TENSOR_PAIRS // CHUNK_PAIRS):
                sums[c] = ps_acc.tile([P, PACK, CHUNK_PAIRS], F32, name="acc")
            for c in range(TENSOR_PAIRS // CHUNK_PAIRS):
                for t in range(PACK):
                    nc.tensor.matmul(
                        out=sums[c][:, t, :],
                        lhsT=xi_aug[:, 0, K_PASS * g + t : K_PASS * (g + 1) : PACK],
                        rhs=pair_pick[:, c * CHUNK_PAIRS : (c + 1) * CHUNK_PAIRS],
                        start=True,
                        stop=True,
                    )
            for c in range(TENSOR_PAIRS // CHUNK_PAIRS):
                nc.scalar.activation(
                    out=h_of[(0, g)][:, c * CHUNK_PAIRS * PACK : (c + 1) * CHUNK_PAIRS * PACK].rearrange(
                        "p (n t) -> p n t", t=PACK
                    ),
                    in_=sums[c][:].rearrange("p t n -> p n t"),
                    func=ACT.Relu,
                )

        def on_vector(unit):
            return unit % VECTOR_RELU_EVERY == VECTOR_RELU_EVERY - 1 or unit == UNITS - 1

        def relu(grp, g):
            h = h_of[(grp, g)][:, first_graph(grp) * NODES * NODES * PACK :]
            if on_vector(grp * PASSES + g):
                nc.vector.tensor_scalar_max(out=h, in0=h, scalar1=0.0)
            else:
                nc.scalar.activation(out=h, in_=h, func=ACT.Relu)

        def quantise(grp, g):
            codes = deep.tile([P, GROUP_PAIRS], U32, name="codes", align_bytes=64)
            scales = deep.tile([P, GROUP_PAIRS], U8, name="scales", align_bytes=64)
            codes_of[(grp, g)] = codes
            scales_of[(grp, g)] = scales
            nc.vector.quantize_mx(out=codes[:].bitcast(FP8X4), scales=scales[:], in_=h_of[(grp, g)][:])

        def multiply(grp, g):
            for half in range(GROUP_BANKS):
                bank = grp * GROUP_BANKS + half
                if g == 0:
                    acc_of[bank] = ps_acc.tile([P, BANK_PAIRS], F32, name="acc")
                first = half * BANK_PAIRS
                nc.tensor.matmul_mx(
                    out=acc_of[bank][:],
                    lhsT=w_words[:, g, :].bitcast(FP4X4),
                    lhsT_scale=w_scales[:, g, :],
                    rhs=codes_of[(grp, g)][:, first : first + BANK_PAIRS].bitcast(FP8X4),
                    rhs_scale=scales_of[(grp, g)][:, first : first + BANK_PAIRS],
                    start=(g == 0),
                    stop=(g == PASSES - 1),
                )

        def empty_bank(bank):
            nt, place = divmod(bank, NODE_BANKS)
            if place == 0:
                msgs_of[nt] = work.tile([P, NODES, NODE_TILE], F32, name="msgs")
            rows = msgs_of[nt][:, :, place * BANK_ROWS : (place + 1) * BANK_ROWS]
            products = acc_of[bank][:].rearrange("p (r j) -> p j r", j=NODES)
            if bank == BANKS - 1:
                nc.vector.tensor_scalar(
                    out=rows, in0=products, scalar1=bias_col[:, 0:1], scalar2=0.0, op0=ALU.add, op1=ALU.max
                )
            else:
                nc.scalar.activation(out=rows, in_=products, func=ACT.Relu, bias=bias_col[:, 0:1])

        def sum_senders(nt):
            total = ps_misc.tile([P, OUT_DIM], F32, name="total", tag="misc")
            total_of[nt] = total
            nc.tensor.matmul(
                out=total[:],
                lhsT=surplus[:, nt * TILE_GRAPHS : (nt + 1) * TILE_GRAPHS, :].rearrange("p b i -> p (b i)"),
                rhs=ident_f32[:],
                start=True,
                stop=False,
                is_transpose=True,
            )
            for j in range(NODES):
                nc.tensor.matmul(
                    out=total[:],
                    lhsT=msgs_of[nt][:, j, :],
                    rhs=ident_f32[:],
                    start=False,
                    stop=(j == NODES - 1),
                    is_transpose=True,
                )

        def finish(nt):
            result = work.tile([P, OUT_DIM], F32, name="result")
            nc.scalar.copy(out=result[:], in_=total_of[nt][:])
            nc.sync.dma_start(out=out_rows[nt * NODE_TILE : (nt + 1) * NODE_TILE, :], in_=result[:])

        spread_of = {}

        def surplus_constants():
            nc.vector.memset(first_row[:], 0.0)
            nc.vector.memset(first_row[0:1, :], 1.0)
            nc.vector.tensor_reduce(
                out=same_graph[:],
                in_=ident_f32[:].rearrange("p (b j) -> p b j", j=NODES),
                axis=AXIS.X,
                op=ALU.add,
            )

        def begin_surplus():
            spread = ps_misc.tile([P, OUT_DIM], F32, name="spread", tag="misc")
            spread_of[0] = spread
            nc.tensor.matmul(out=spread[:], lhsT=first_row[:], rhs=small[:], start=True, stop=True)
            shape = [P, N_NODE_TILES, TILE_GRAPHS]
            nc.vector.tensor_tensor(
                out=sel[:],
                in0=keep_col[:].unsqueeze(2).broadcast_to(shape),
                in1=same_graph[:].unsqueeze(1).broadcast_to(shape),
                op=ALU.mult,
            )

        def end_surplus():
            nc.vector.tensor_scalar_max(out=relu_rows[:], in0=spread_of[0][:], scalar1=0.0)
            share = ps_misc.tile([P, GRAPHS], F32, name="share", tag="misc")
            nc.tensor.matmul(
                out=share[:],
                lhsT=relu_rows[:],
                rhs=sel[:].rearrange("p n b -> p (n b)"),
                start=True,
                stop=True,
            )
            nc.scalar.activation(
                out=surplus[:],
                in_=share[:].unsqueeze(2).broadcast_to([P, GRAPHS, NODES]),
                func=ACT.Identity,
                bias=all_padded[:, 0:1],
            )

        def prepare(grp):
            prepare_receivers(grp)
            if grp % 2 == 0:
                mask_senders(grp // 2)
                turn_senders(grp // 2)

        def copy_prepared(grp):
            if grp % 2 == 0:
                copy_senders(grp // 2)
            copy_receivers(grp)

        build_pair_pick()
        surplus_constants()
        mask_factors(0, 1, first_mask[:, 0:1])
        prepare(0)
        copy_prepared(0)
        pool_add(0, 0)
        turn_small()
        mask_moved_senders()
        tensor_add(0)
        prepare(1)
        copy_prepared(1)
        pool_add(0, 1)
        read_small()
        begin_surplus()
        for v in range(N_GROUPS + 3):
            if v + 1 < N_GROUPS:
                for g in range(PASSES):
                    pool_add(v + 1, g)
            if v < N_GROUPS:
                for g in range(PASSES):
                    vector_add(v, g)
                    if not on_vector(v * PASSES + g):
                        relu(v, g)
                    if v == 0 and g == 0:
                        tensor_add(1)
                        load_receivers(XI_SLOTS)
            if 1 <= v <= N_GROUPS:
                for g in range(PASSES):
                    if on_vector((v - 1) * PASSES + g):
                        relu(v - 1, g)
            if v == 0:
                end_surplus()
            if v + 2 < N_GROUPS:
                prepare(v + 2)
            if 1 <= v <= N_GROUPS:
                for g in range(PASSES):
                    quantise(v - 1, g)
                    multiply(v - 1, g)
            if v + 2 < N_GROUPS:
                copy_prepared(v + 2)
            if 2 <= v < N_GROUPS + 2:
                for half in range(GROUP_BANKS):
                    empty_bank((v - 2) * GROUP_BANKS + half)
            if v >= 3 and v % 2 == 1:
                sum_senders((v - 3) // 2)
            if v >= 4 and v % 2 == 0:
                finish((v - 4) // 2)
